import numpy as np
import ml_dtypes


def mxq(x, axis, fmt="e4m3"):
    dtype, down = {"e4m3": (ml_dtypes.float8_e4m3fn, 7), "e5m2": (ml_dtypes.float8_e5m2, 14)}[fmt]
    v = np.moveaxis(np.asarray(x, np.float32).astype(ml_dtypes.bfloat16).astype(np.float64), axis, -1)
    blocks = v.reshape(v.shape[:-1] + (-1, 32))
    amax = np.abs(blocks).max(-1, keepdims=True)
    byte = np.maximum(np.where(amax > 0, np.frexp(amax)[1] - 1 + 127, 0) - down, 1)
    scale = np.exp2(byte - 127.0)
    codes = (blocks / scale).astype(np.float32).astype(dtype).astype(np.float64)
    return np.moveaxis((codes * scale).reshape(v.shape), -1, axis)


WIDE = False


def mx_kscale(k):
    if not WIDE:
        return np.ones(k)
    levels = np.array([10, -10, 5, -5, 0])
    a = np.random.permutation(np.resize(levels, k // 512 * 4)).reshape(k // 512, 4)
    idx = np.arange(k)
    return np.exp2(a[idx // 512, idx % 128 // 32])


BF16 = ml_dtypes.bfloat16


def bf(x):
    return np.asarray(x, np.float32).astype(BF16)


def f64(x):
    return np.asarray(x).astype(np.float64)


E2M1 = np.array([0.0, 0.5, 1.0, 1.5, 2.0, 3.0, 4.0, 6.0, -0.0, -0.5, -1.0, -1.5, -2.0, -3.0, -4.0, -6.0])


def pack_weight(w, fmt):
    k, n = w.shape
    w = f64(bf(w)).reshape(k // 32, 32, n)
    amax = np.abs(w).max(1)
    if fmt == "e4m3":
        byte = np.frexp(amax)[1] - 1 + 127 - 7
    else:
        mant, ex = np.frexp(amax / 6.0)
        byte = np.where(mant > 0.5, ex, ex - 1) + 127
    byte = np.clip(np.where(amax > 0, byte, 1), 1, 254)
    scaled = (w * np.exp2(127.0 - byte)[:, None, :]).reshape(k, n).astype(np.float32)
    by_word = np.ascontiguousarray(scaled.reshape(k // 512, 128, 4, n).transpose(0, 1, 3, 2))
    if fmt == "e4m3":
        words = by_word.astype(ml_dtypes.float8_e4m3fn).view(np.uint8)
    else:
        c = by_word.astype(ml_dtypes.float4_e2m1fn).view(np.uint8) & 0xF
        words = c[..., 0::2] | (c[..., 1::2] << 4)
    return np.ascontiguousarray(words), np.ascontiguousarray(byte.astype(np.uint8).reshape(k // 512, 16, n))


def unpack_weight(words, scales, fmt):
    g, p, n, _ = words.shape
    if fmt == "e4m3":
        vals = np.ascontiguousarray(words).view(ml_dtypes.float8_e4m3fn).astype(np.float64)
    else:
        nib = np.empty((g, p, n, 4), np.uint8)
        nib[..., 0::2] = words & 0xF
        nib[..., 1::2] = words >> 4
        vals = E2M1[nib]
    vals = vals * np.repeat(np.exp2(scales.astype(np.float64) - 127.0), 8, axis=1)[..., None]
    return vals.transpose(0, 1, 3, 2).reshape(g * 512, n)


B, S, K, IN, HID, OUT = 4, 128, 16, 1024, 512, 127
LN_EPS = 1e-5
LINK_EPS = 1e-8
FMT = "e4m3"


def sigmoid(v):
    return 1.0 / (1.0 + np.exp(-v))


def setup_inputs():
    s, t = mx_kscale(IN), mx_kscale(HID)
    keep = np.random.random((B, S, 1, 1)) > 0.125
    net_in = bf(np.random.standard_normal((B, S, K, IN)) * s)
    embeds = bf(np.random.standard_normal((B, S, OUT)) * 0.5)
    m = bf(np.random.random((B, S, K, 1)) * keep)
    W1_words, W1_scales = pack_weight(np.random.standard_normal((IN, HID)) / np.sqrt(IN) / s[:, None] * t, FMT)
    b1 = bf(np.random.standard_normal(HID) * 0.3 * t)
    Wf_words, Wf_scales = pack_weight(np.random.standard_normal((HID, OUT + 1)) * 3.0 / np.sqrt(HID) / t[:, None], FMT)
    b_f = bf(np.random.standard_normal(OUT + 1) * 0.3)
    gamma = bf(1.0 + 0.1 * np.random.standard_normal(OUT))
    beta = bf(0.1 * np.random.standard_normal(OUT))
    return {"net_in": net_in,
            "embeds": embeds,
            "m": m,
            "W1_words": W1_words,
            "W1_scales": W1_scales,
            "b1": b1,
            "Wf_words": Wf_words,
            "Wf_scales": Wf_scales,
            "b_f": b_f,
            "gamma": gamma,
            "beta": beta}


def reference(net_in, embeds, m, W1_words, W1_scales, b1, Wf_words, Wf_scales, b_f, gamma, beta):
    h = np.maximum((mxq(f64(net_in), 3, "e4m3") @ unpack_weight(W1_words, W1_scales, FMT)) + f64(b1), 0.0)
    out = (mxq(h, 3, "e4m3") @ unpack_weight(Wf_words, Wf_scales, FMT)) + f64(b_f)
    out = np.concatenate([out[..., :-1], sigmoid(out[..., -1:])], axis=-1)
    out = f64(m) * out
    link_weight = out[..., -1] + LINK_EPS
    norm = link_weight.sum(axis=2, keepdims=True)
    weights = (link_weight / norm)[..., None]
    updates = (out * weights).sum(axis=2)
    upd_weights = updates[..., -1:]
    embeds_new = f64(embeds) + upd_weights * updates[..., :-1]
    mu = embeds_new.mean(axis=-1, keepdims=True)
    var = ((embeds_new - mu) ** 2).mean(axis=-1, keepdims=True)
    return (embeds_new - mu) / np.sqrt(var + LN_EPS) * f64(gamma) + f64(beta)

@@ -1,0 +1,350 @@
+from contextlib import ExitStack
+
+import concourse.mybir as mybir
+from concourse.masks import make_identity
+
+F32 = mybir.dt.float32
+BF16 = mybir.dt.bfloat16
+I32 = mybir.dt.int32
+U8 = mybir.dt.uint8
+U32 = mybir.dt.uint32
+FP8X4 = mybir.dt.float8_e4m3fn_x4
+ALU = mybir.AluOpType
+ACT = mybir.ActivationFunctionType
+AXIS = mybir.AxisListType
+
+P = 128
+BATCHES, LINKS, IN, HID, CHANNELS = 4, 16, 1024, 512, 128
+FEATURES = CHANNELS - 1
+K_PASS = 4 * P
+IN_PASSES = IN // K_PASS
+LN_EPS = 1e-5
+LINK_EPS = 1e-8
+
+ROUND_TILES = 2
+ROUNDS = BATCHES * LINKS // ROUND_TILES
+ROUNDS_PER_BATCH = LINKS // ROUND_TILES
+LOADS_AHEAD = 6
+LAST_LAG = 8
+
+FLOPS = 2 * BATCHES * P * LINKS * (IN * HID + HID * CHANNELS)
+
+
+def tile_embed_update_pa_t_kernel(
+    tc, net_in, embeds, m, W1_words, W1_scales, b1, Wf_words, Wf_scales, b_f, gamma, beta, out
+):
+    nc = tc.nc
+    with ExitStack() as ctx:
+        ctx.enter_context(tc.manual_schedule())
+        const = ctx.enter_context(tc.tile_pool(name="const", bufs=1))
+        x_pool = ctx.enter_context(tc.tile_pool(name="x", bufs=LOADS_AHEAD))
+        stage = ctx.enter_context(tc.tile_pool(name="stage", bufs=2))
+        rows_pool = ctx.enter_context(tc.tile_pool(name="rows", bufs=3 * ROUND_TILES))
+        finish_pool = ctx.enter_context(tc.tile_pool(name="finish", bufs=2))
+        xt_pool = ctx.enter_context(tc.psum_pool(name="xt", bufs=2))
+        acc_pool = ctx.enter_context(tc.psum_pool(name="acc", bufs=3))
+        ht_pool = ctx.enter_context(tc.psum_pool(name="ht", bufs=1))
+        o_pool = ctx.enter_context(tc.psum_pool(name="o", bufs=2))
+
+        x_tiles = {}
+
+        def load_x(r):
+            batch, first_link = divmod(r * ROUND_TILES, LINKS)
+            x_rows = x_pool.tile([P, ROUND_TILES, IN], BF16)
+            nc.sync.dma_start(
+                out=x_rows[:], in_=net_in[batch, :, first_link : first_link + ROUND_TILES, :]
+            )
+            x_tiles[r] = x_rows
+
+        load_x(0)
+
+        w1_scales = const.tile([P, IN_PASSES, HID], U8, align_bytes=64)
+        wf_scales = const.tile([P, CHANNELS], U8, align_bytes=64)
+        nc.vector.memset(w1_scales[:].rearrange("p g n -> p (g n)").bitcast(I32), 0)
+        nc.vector.memset(wf_scales[:].bitcast(I32), 0)
+        for quadrant in range(4):
+            live = slice(32 * quadrant, 32 * quadrant + 4)
+            rows = slice(4 * quadrant, 4 * quadrant + 4)
+            nc.sync.dma_start(
+                out=w1_scales[live, :, :].bitcast(I32),
+                in_=W1_scales[:, rows, :].rearrange("g r n -> r g n").bitcast(I32),
+            )
+            nc.sync.dma_start(out=wf_scales[live, :].bitcast(I32), in_=Wf_scales[0, rows, :].bitcast(I32))
+        w1_words = const.tile([P, IN_PASSES, 4 * HID], U8, align_bytes=64)
+        for g in range(IN_PASSES):
+            nc.sync.dma_start(
+                out=w1_words[:, g, :].bitcast(I32),
+                in_=W1_words[g].rearrange("p n t -> p (n t)").bitcast(I32),
+            )
+        wf_words = const.tile([P, 4 * CHANNELS], U8, align_bytes=64)
+        nc.sync.dma_start(
+            out=wf_words[:].bitcast(I32), in_=Wf_words[0].rearrange("p n t -> p (n t)").bitcast(I32)
+        )
+        for r in range(1, LOADS_AHEAD):
+            load_x(r)
+
+        identity = const.tile([P, P], F32)
+        make_identity(nc, identity[:])
+        minus_half = const.tile([P, 1], F32)
+        nc.gpsimd.memset(minus_half[:], -0.5)
+        table_warmer = const.tile([P, 1], F32)
+        nc.scalar.activation(out=table_warmer[:], in_=minus_half[:], func=ACT.Sigmoid)
+
+        b1_bf = const.tile([P, HID], BF16)
+        nc.scalar.dma_start(out=b1_bf[:], in_=b1.partition_broadcast(P))
+        bf_bf = const.tile([P, CHANNELS], BF16)
+        nc.scalar.dma_start(out=bf_bf[:], in_=b_f.partition_broadcast(P))
+        gamma_bf = const.tile([P, FEATURES], BF16)
+        nc.scalar.dma_start(out=gamma_bf[:], in_=gamma.partition_broadcast(P))
+        beta_bf = const.tile([P, FEATURES], BF16)
+        nc.scalar.dma_start(out=beta_bf[:], in_=beta.partition_broadcast(P))
+        m_bf = const.tile([P, BATCHES, LINKS], BF16)
+        nc.scalar.dma_start(out=m_bf[:], in_=m.rearrange("b s k o -> s b (k o)"))
+        embeds_bf = const.tile([P, BATCHES, FEATURES], BF16)
+        nc.scalar.dma_start(out=embeds_bf[:], in_=embeds.rearrange("b s c -> s b c"))
+
+        b1_sorted = const.tile([P, HID], F32)
+        nc.vector.tensor_copy(
+            out=b1_sorted[:].rearrange("t (u q e) -> t u q e", u=2, e=2),
+            in_=b1_bf[:].rearrange("t (q u e) -> t u q e", u=2, e=2),
+        )
+        bf_f32 = const.tile([P, CHANNELS], F32)
+        nc.vector.tensor_copy(out=bf_f32[:], in_=bf_bf[:])
+        m_f32 = const.tile([P, BATCHES * LINKS], F32)
+        nc.vector.tensor_copy(out=m_f32[:], in_=m_bf[:].rearrange("s b k -> s (b k)"))
+        sigmoid = const.tile([P, BATCHES * LINKS], F32)
+        g_link = const.tile([P, BATCHES * LINKS], F32)
+        L, L_M, L_G = 0, 1, 2
+        terms = const.tile([P, 3, BATCHES * LINKS], F32)
+
+        xt_tiles, xq_tiles, acc_tiles, h_rows_tiles = {}, {}, {}, {}
+        ht_tiles, hg_tiles, hq_tiles, o_tiles, sum_tiles = {}, {}, {}, {}, {}
+
+        def transpose_x(r):
+            for i in range(ROUND_TILES):
+                words = x_tiles[r][:, i, :].bitcast(F32)
+                x_t = xt_pool.tile([P, 2 * IN_PASSES, P], F32)
+                for g in range(IN_PASSES):
+                    for u in range(2):
+                        first = g * (K_PASS // 2) + u
+                        nc.tensor.transpose(
+                            x_t[:, 2 * g + u, :], words[:, first : (g + 1) * (K_PASS // 2) : 2], identity[:]
+                        )
+                xt_tiles[r, i] = x_t
+
+        def group_x(r):
+            x_grouped = stage.tile([P, ROUND_TILES, IN_PASSES, P, 4], BF16, align_bytes=64)
+            for i in range(ROUND_TILES):
+                nc.scalar.copy(
+                    out=x_grouped[:, i].bitcast(F32),
+                    in_=xt_tiles[r, i][:].rearrange("p (g u) t -> p g t u", u=2),
+                )
+            return x_grouped
+
+        def quantise_x(r, x_grouped):
+            x_codes = stage.tile([P, ROUND_TILES, IN_PASSES, P], U32, align_bytes=64)
+            x_scales = stage.tile([P, ROUND_TILES, IN_PASSES, P], U8, align_bytes=64)
+            nc.vector.quantize_mx(
+                out=x_codes[:].rearrange("p i g t -> p (i g t)").bitcast(FP8X4),
+                scales=x_scales[:].rearrange("p i g t -> p (i g t)"),
+                in_=x_grouped[:].rearrange("p i g t j -> p (i g t j)"),
+            )
+            xq_tiles[r] = (x_codes, x_scales)
+
+        def first_matmul(r):
+            x_codes, x_scales = xq_tiles[r]
+            for i in range(ROUND_TILES):
+                acc = acc_pool.tile([P, HID], F32)
+                for g in range(IN_PASSES):
+                    nc.tensor.matmul_mx(
+                        out=acc[:],
+                        lhsT=x_codes[:, i, g, :].bitcast(FP8X4),
+                        lhsT_scale=x_scales[:, i, g, :],
+                        rhs=w1_words[:, g, :].bitcast(FP8X4),
+                        rhs_scale=w1_scales[:, g, :],
+                        start=(g == 0),
+                        stop=(g == IN_PASSES - 1),
+                    )
+                acc_tiles[r, i] = acc
+
+        def add_bias(r):
+            for i in range(ROUND_TILES):
+                h_rows = rows_pool.tile([P, HID], BF16)
+                nc.vector.tensor_tensor(
+                    out=h_rows[:].rearrange("t (u q e) -> t u q e", u=2, e=2),
+                    in0=acc_tiles[r, i][:].rearrange("t (q u e) -> t u q e", u=2, e=2),
+                    in1=b1_sorted[:].rearrange("t (u q e) -> t u q e", u=2, e=2),
+                    op=ALU.add,
+                )
+                h_rows_tiles[r, i] = h_rows
+
+        def transpose_h(r):
+            h_t = ht_pool.tile([P, ROUND_TILES, 2, P], F32)
+            for i in range(ROUND_TILES):
+                words = h_rows_tiles[r, i][:].bitcast(F32)
+                for u in range(2):
+                    nc.tensor.transpose(h_t[:, i, u, :], words[:, u * P : (u + 1) * P], identity[:])
+            ht_tiles[r] = h_t
+
+        def relu_and_group_h(r):
+            h_grouped = stage.tile([P, ROUND_TILES, P, 4], BF16, align_bytes=64)
+            for i in range(ROUND_TILES):
+                nc.scalar.activation(
+                    out=h_grouped[:, i].rearrange("p t (u e) -> p t u e", u=2),
+                    in_=ht_tiles[r][:, i].bitcast(BF16).rearrange("p u (t e) -> p t u e", e=2),
+                    func=ACT.Relu,
+                )
+            hg_tiles[r] = h_grouped
+
+        def quantise_h(r):
+            h_codes = stage.tile([P, ROUND_TILES, P], U32, align_bytes=64)
+            h_scales = stage.tile([P, ROUND_TILES, P], U8, align_bytes=64)
+            nc.vector.quantize_mx(
+                out=h_codes[:].rearrange("p i t -> p (i t)").bitcast(FP8X4),
+                scales=h_scales[:].rearrange("p i t -> p (i t)"),
+                in_=hg_tiles[r][:].rearrange("p i t j -> p (i t j)"),
+            )
+            hq_tiles[r] = (h_codes, h_scales)
+
+        def second_matmul(r):
+            h_codes, h_scales = hq_tiles[r]
+            o = o_pool.tile([P, ROUND_TILES, CHANNELS], F32)
+            for i in range(ROUND_TILES):
+                nc.tensor.matmul_mx(
+                    out=o[:, i, :],
+                    lhsT=h_codes[:, i, :].bitcast(FP8X4),
+                    lhsT_scale=h_scales[:, i, :],
+                    rhs=wf_words[:].bitcast(FP8X4),
+                    rhs_scale=wf_scales[:],
+                    start=True,
+                    stop=True,
+                )
+            o_tiles[r] = o
+
+        def gate(r):
+            cols = slice(r * ROUND_TILES, (r + 1) * ROUND_TILES)
+            nc.scalar.activation(
+                out=sigmoid[:, cols],
+                in_=o_tiles[r][:, :, FEATURES],
+                func=ACT.Sigmoid,
+                bias=bf_f32[:, FEATURES:CHANNELS],
+            )
+            nc.gpsimd.tensor_tensor(out=g_link[:, cols], in0=sigmoid[:, cols], in1=m_f32[:, cols], op=ALU.mult)
+            nc.gpsimd.tensor_scalar(
+                out=terms[:, L, cols], in0=g_link[:, cols], scalar1=LINK_EPS, scalar2=1.0,
+                op0=ALU.add, op1=ALU.mult,
+            )
+            nc.gpsimd.tensor_tensor(out=terms[:, L_M, cols], in0=terms[:, L, cols], in1=m_f32[:, cols], op=ALU.mult)
+            nc.gpsimd.tensor_tensor(out=terms[:, L_G, cols], in0=terms[:, L, cols], in1=g_link[:, cols], op=ALU.mult)
+
+        def add_links(r):
+            batch, round_in_batch = divmod(r, ROUNDS_PER_BATCH)
+            if round_in_batch == 0:
+                link_sums = finish_pool.tile([P, ROUND_TILES, CHANNELS], F32)
+                sum_tiles[batch] = link_sums
+            for i in range(ROUND_TILES):
+                weight = terms[:, L_M, r * ROUND_TILES + i : r * ROUND_TILES + i + 1]
+                if round_in_batch == 0:
+                    nc.vector.tensor_scalar(
+                        out=sum_tiles[batch][:, i, :], in0=o_tiles[r][:, i, :],
+                        scalar1=weight, scalar2=None, op0=ALU.mult,
+                    )
+                else:
+                    nc.vector.scalar_tensor_tensor(
+                        out=sum_tiles[batch][:, i, :], in0=o_tiles[r][:, i, :], scalar=weight,
+                        in1=sum_tiles[batch][:, i, :], op0=ALU.mult, op1=ALU.add,
+                    )
+
+        update_tiles, e_tiles, norm_tiles = {}, {}, {}
+
+        def finish_update(batch):
+            sums = finish_pool.tile([P, 3], F32)
+            nc.vector.tensor_reduce(
+                out=sums[:], in_=terms[:, :, batch * LINKS : (batch + 1) * LINKS], axis=AXIS.X, op=ALU.add
+            )
+            inv_l = finish_pool.tile([P, 1], F32)
+            nc.vector.reciprocal(out=inv_l[:], in_=sums[:, L : L + 1])
+            factor = finish_pool.tile([P, 1], F32)
+            nc.vector.tensor_scalar(
+                out=factor[:], in0=sums[:, L_G : L_G + 1], scalar1=inv_l[:], scalar2=inv_l[:],
+                op0=ALU.mult, op1=ALU.mult,
+            )
+            link_sums = sum_tiles[batch]
+            update = finish_pool.tile([P, FEATURES], F32)
+            nc.vector.scalar_tensor_tensor(
+                out=update[:], in0=bf_f32[:, 0:FEATURES], scalar=sums[:, L_M : L_M + 1],
+                in1=link_sums[:, 0, 0:FEATURES], op0=ALU.mult, op1=ALU.add,
+            )
+            nc.vector.tensor_tensor(
+                out=update[:], in0=update[:], in1=link_sums[:, 1, 0:FEATURES], op=ALU.add
+            )
+            update_tiles[batch] = (update, factor)
+
+        def finish_statistics(batch):
+            update, factor = update_tiles[batch]
+            e = finish_pool.tile([P, FEATURES], F32)
+            nc.vector.scalar_tensor_tensor(
+                out=e[:], in0=update[:], scalar=factor[:], in1=embeds_bf[:, batch, :],
+                op0=ALU.mult, op1=ALU.add,
+            )
+            stats = finish_pool.tile([P, 6], F32)
+            nc.vector.bn_stats(out=stats[:], in_=e[:])
+            mean_var = finish_pool.tile([P, 2], F32)
+            nc.vector.bn_aggr(out=mean_var[:], in_=stats[:])
+            var_eps = finish_pool.tile([P, 1], F32)
+            nc.gpsimd.tensor_scalar(
+                out=var_eps[:], in0=mean_var[:, 1:2], scalar1=LN_EPS, scalar2=1.0, op0=ALU.add, op1=ALU.mult
+            )
+            inv_std = finish_pool.tile([P, 1], F32)
+            nc.gpsimd.tensor_tensor(out=inv_std[:], in0=var_eps[:], in1=minus_half[:], op=ALU.pow)
+            e_tiles[batch] = e
+            norm_tiles[batch] = (mean_var, inv_std)
+
+        def finish_norm(batch):
+            mean_var, inv_std = norm_tiles[batch]
+            centred = finish_pool.tile([P, FEATURES], F32)
+            nc.vector.scalar_tensor_tensor(
+                out=centred[:], in0=e_tiles[batch][:], scalar=mean_var[:, 0:1], in1=gamma_bf[:],
+                op0=ALU.subtract, op1=ALU.mult,
+            )
+            result = finish_pool.tile([P, FEATURES], F32)
+            nc.vector.scalar_tensor_tensor(
+                out=result[:], in0=centred[:], scalar=inv_std[:], in1=beta_bf[:],
+                op0=ALU.mult, op1=ALU.add,
+            )
+            nc.sync.dma_start(out=out[batch], in_=result[:])
+
+        def in_range(r):
+            return 0 <= r < ROUNDS
+
+        def ends_batch(r):
+            return in_range(r) and r % ROUNDS_PER_BATCH == ROUNDS_PER_BATCH - 1
+
+        for i in range(ROUNDS + LAST_LAG):
+            x_grouped = None
+            if in_range(i):
+                transpose_x(i)
+                x_grouped = group_x(i)
+            if in_range(i + LOADS_AHEAD):
+                load_x(i + LOADS_AHEAD)
+            if in_range(i - 3):
+                transpose_h(i - 3)
+                relu_and_group_h(i - 3)
+            if in_range(i - 4):
+                quantise_h(i - 4)
+            if in_range(i - 6):
+                add_links(i - 6)
+            if ends_batch(i - 6):
+                finish_update((i - 6) // ROUNDS_PER_BATCH)
+            if ends_batch(i - 7):
+                finish_statistics((i - 7) // ROUNDS_PER_BATCH)
+            if ends_batch(i - LAST_LAG):
+                finish_norm((i - LAST_LAG) // ROUNDS_PER_BATCH)
+            if in_range(i):
+                quantise_x(i, x_grouped)
+            if in_range(i - 1):
+                first_matmul(i - 1)
+                add_bias(i - 1)
+            if in_range(i - 4):
+                second_matmul(i - 4)
+                gate(i - 4)

@@ -56,62 +56,57 @@ def tile_embed_update_pa_t_kernel(
             )
             x_tiles[r] = x_rows
 
-        load_x(0)
+        identity = const.tile([P, P], F32)
+        make_identity(nc, identity[:])
+        minus_half = const.tile([P, 1], F32)
+        nc.gpsimd.memset(minus_half[:], -0.5)
+        minus_one = const.tile([P, 1], F32)
+        nc.gpsimd.memset(minus_one[:], -1.0)
+        table_warmer = const.tile([P, 1], F32)
+        nc.scalar.activation(out=table_warmer[:], in_=minus_half[:], func=ACT.Sigmoid)
 
         w1_scales = const.tile([P, IN_PASSES, HID], U8, align_bytes=64)
         wf_scales = const.tile([P, CHANNELS], U8, align_bytes=64)
         nc.vector.memset(w1_scales[:].rearrange("p g n -> p (g n)").bitcast(I32), 0)
         nc.vector.memset(wf_scales[:].bitcast(I32), 0)
-        for quadrant in range(4):
-            live = slice(32 * quadrant, 32 * quadrant + 4)
-            rows = slice(4 * quadrant, 4 * quadrant + 4)
-            nc.sync.dma_start(
-                out=w1_scales[live, :, :].bitcast(I32),
-                in_=W1_scales[:, rows, :].rearrange("g r n -> r g n").bitcast(I32),
-            )
-            nc.sync.dma_start(out=wf_scales[live, :].bitcast(I32), in_=Wf_scales[0, rows, :].bitcast(I32))
+
+        def load_scales(plane, scale_rows):
+            for quadrant in range(4):
+                nc.sync.dma_start(
+                    out=plane[32 * quadrant : 32 * quadrant + 4].bitcast(I32),
+                    in_=scale_rows[4 * quadrant : 4 * quadrant + 4].bitcast(I32),
+                )
+
+        load_x(0)
+        load_scales(w1_scales, W1_scales.rearrange("g r n -> r g n"))
+        load_x(1)
         w1_words = const.tile([P, IN_PASSES, 4 * HID], U8, align_bytes=64)
-        for g in range(IN_PASSES):
-            nc.sync.dma_start(
-                out=w1_words[:, g, :].bitcast(I32),
-                in_=W1_words[g].rearrange("p n t -> p (n t)").bitcast(I32),
-            )
+        nc.sync.dma_start(
+            out=w1_words[:].bitcast(I32), in_=W1_words.rearrange("g p n t -> p g (n t)").bitcast(I32)
+        )
+        b1_bf = const.tile([P, HID], BF16)
+        nc.sync.dma_start(out=b1_bf[:], in_=b1.partition_broadcast(P))
+        load_x(2)
         wf_words = const.tile([P, 4 * CHANNELS], U8, align_bytes=64)
         nc.sync.dma_start(
             out=wf_words[:].bitcast(I32), in_=Wf_words[0].rearrange("p n t -> p (n t)").bitcast(I32)
         )
-        for r in range(1, LOADS_AHEAD):
-            load_x(r)
-
-        identity = const.tile([P, P], F32)
-        make_identity(nc, identity[:])
-        minus_half = const.tile([P, 1], F32)
-        nc.gpsimd.memset(minus_half[:], -0.5)
-        table_warmer = const.tile([P, 1], F32)
-        nc.scalar.activation(out=table_warmer[:], in_=minus_half[:], func=ACT.Sigmoid)
-
-        b1_bf = const.tile([P, HID], BF16)
-        nc.scalar.dma_start(out=b1_bf[:], in_=b1.partition_broadcast(P))
+        load_scales(wf_scales, Wf_scales[0])
+        load_x(3)
         bf_bf = const.tile([P, CHANNELS], BF16)
-        nc.scalar.dma_start(out=bf_bf[:], in_=b_f.partition_broadcast(P))
-        gamma_bf = const.tile([P, FEATURES], BF16)
-        nc.scalar.dma_start(out=gamma_bf[:], in_=gamma.partition_broadcast(P))
-        beta_bf = const.tile([P, FEATURES], BF16)
-        nc.scalar.dma_start(out=beta_bf[:], in_=beta.partition_broadcast(P))
+        nc.sync.dma_start(out=bf_bf[:], in_=b_f.partition_broadcast(P))
         m_bf = const.tile([P, BATCHES, LINKS], BF16)
-        nc.scalar.dma_start(out=m_bf[:], in_=m.rearrange("b s k o -> s b (k o)"))
+        nc.sync.dma_start(out=m_bf[:], in_=m.rearrange("b s k o -> s b (k o)"))
+        for r in range(4, LOADS_AHEAD):
+            load_x(r)
+        gamma_bf = const.tile([P, FEATURES], BF16)
+        nc.sync.dma_start(out=gamma_bf[:], in_=gamma.partition_broadcast(P))
+        beta_bf = const.tile([P, FEATURES], BF16)
+        nc.sync.dma_start(out=beta_bf[:], in_=beta.partition_broadcast(P))
         embeds_bf = const.tile([P, BATCHES, FEATURES], BF16)
-        nc.scalar.dma_start(out=embeds_bf[:], in_=embeds.rearrange("b s c -> s b c"))
+        nc.sync.dma_start(out=embeds_bf[:], in_=embeds.rearrange("b s c -> s b c"))
 
-        b1_sorted = const.tile([P, HID], F32)
-        nc.vector.tensor_copy(
-            out=b1_sorted[:].rearrange("t (u q e) -> t u q e", u=2, e=2),
-            in_=b1_bf[:].rearrange("t (q u e) -> t u q e", u=2, e=2),
-        )
-        bf_f32 = const.tile([P, CHANNELS], F32)
-        nc.vector.tensor_copy(out=bf_f32[:], in_=bf_bf[:])
-        m_f32 = const.tile([P, BATCHES * LINKS], F32)
-        nc.vector.tensor_copy(out=m_f32[:], in_=m_bf[:].rearrange("s b k -> s (b k)"))
+        m_link = m_bf[:].rearrange("s b k -> s (b k)")
         sigmoid = const.tile([P, BATCHES * LINKS], F32)
         g_link = const.tile([P, BATCHES * LINKS], F32)
         L, L_M, L_G = 0, 1, 2
@@ -173,7 +168,7 @@ def tile_embed_update_pa_t_kernel(
                 nc.vector.tensor_tensor(
                     out=h_rows[:].rearrange("t (u q e) -> t u q e", u=2, e=2),
                     in0=acc_tiles[r, i][:].rearrange("t (q u e) -> t u q e", u=2, e=2),
-                    in1=b1_sorted[:].rearrange("t (u q e) -> t u q e", u=2, e=2),
+                    in1=b1_bf[:].rearrange("t (q u e) -> t u q e", u=2, e=2),
                     op=ALU.add,
                 )
                 h_rows_tiles[r, i] = h_rows
@@ -227,33 +222,30 @@ def tile_embed_update_pa_t_kernel(
                 out=sigmoid[:, cols],
                 in_=o_tiles[r][:, :, FEATURES],
                 func=ACT.Sigmoid,
-                bias=bf_f32[:, FEATURES:CHANNELS],
+                bias=bf_bf[:, FEATURES:CHANNELS],
             )
-            nc.gpsimd.tensor_tensor(out=g_link[:, cols], in0=sigmoid[:, cols], in1=m_f32[:, cols], op=ALU.mult)
+            nc.gpsimd.tensor_tensor(out=g_link[:, cols], in0=sigmoid[:, cols], in1=m_link[:, cols], op=ALU.mult)
             nc.gpsimd.tensor_scalar(
                 out=terms[:, L, cols], in0=g_link[:, cols], scalar1=LINK_EPS, scalar2=1.0,
                 op0=ALU.add, op1=ALU.mult,
             )
-            nc.gpsimd.tensor_tensor(out=terms[:, L_M, cols], in0=terms[:, L, cols], in1=m_f32[:, cols], op=ALU.mult)
+            nc.gpsimd.tensor_tensor(out=terms[:, L_M, cols], in0=terms[:, L, cols], in1=m_link[:, cols], op=ALU.mult)
             nc.gpsimd.tensor_tensor(out=terms[:, L_G, cols], in0=terms[:, L, cols], in1=g_link[:, cols], op=ALU.mult)
 
-        def add_links(r):
-            batch, round_in_batch = divmod(r, ROUNDS_PER_BATCH)
-            if round_in_batch == 0:
-                link_sums = finish_pool.tile([P, ROUND_TILES, CHANNELS], F32)
-                sum_tiles[batch] = link_sums
-            for i in range(ROUND_TILES):
-                weight = terms[:, L_M, r * ROUND_TILES + i : r * ROUND_TILES + i + 1]
-                if round_in_batch == 0:
-                    nc.vector.tensor_scalar(
-                        out=sum_tiles[batch][:, i, :], in0=o_tiles[r][:, i, :],
-                        scalar1=weight, scalar2=None, op0=ALU.mult,
-                    )
-                else:
-                    nc.vector.scalar_tensor_tensor(
-                        out=sum_tiles[batch][:, i, :], in0=o_tiles[r][:, i, :], scalar=weight,
-                        in1=sum_tiles[batch][:, i, :], op0=ALU.mult, op1=ALU.add,
-                    )
+        def add_link(r, i):
+            batch, link = divmod(r * ROUND_TILES + i, LINKS)
+            weight = terms[:, L_M, r * ROUND_TILES + i : r * ROUND_TILES + i + 1]
+            if link == 0:
+                link_sum = finish_pool.tile([P, CHANNELS], F32)
+                nc.vector.tensor_scalar(
+                    out=link_sum[:], in0=o_tiles[r][:, i, :], scalar1=weight, scalar2=None, op0=ALU.mult
+                )
+                sum_tiles[batch] = link_sum
+            else:
+                nc.vector.scalar_tensor_tensor(
+                    out=sum_tiles[batch][:], in0=o_tiles[r][:, i, :], scalar=weight,
+                    in1=sum_tiles[batch][:], op0=ALU.mult, op1=ALU.add,
+                )
 
         update_tiles, e_tiles, norm_tiles = {}, {}, {}
 
@@ -263,20 +255,16 @@ def tile_embed_update_pa_t_kernel(
                 out=sums[:], in_=terms[:, :, batch * LINKS : (batch + 1) * LINKS], axis=AXIS.X, op=ALU.add
             )
             inv_l = finish_pool.tile([P, 1], F32)
-            nc.vector.reciprocal(out=inv_l[:], in_=sums[:, L : L + 1])
+            nc.gpsimd.tensor_tensor(out=inv_l[:], in0=sums[:, L : L + 1], in1=minus_one[:], op=ALU.pow)
             factor = finish_pool.tile([P, 1], F32)
-            nc.vector.tensor_scalar(
+            nc.gpsimd.tensor_scalar(
                 out=factor[:], in0=sums[:, L_G : L_G + 1], scalar1=inv_l[:], scalar2=inv_l[:],
                 op0=ALU.mult, op1=ALU.mult,
             )
-            link_sums = sum_tiles[batch]
             update = finish_pool.tile([P, FEATURES], F32)
             nc.vector.scalar_tensor_tensor(
-                out=update[:], in0=bf_f32[:, 0:FEATURES], scalar=sums[:, L_M : L_M + 1],
-                in1=link_sums[:, 0, 0:FEATURES], op0=ALU.mult, op1=ALU.add,
-            )
-            nc.vector.tensor_tensor(
-                out=update[:], in0=update[:], in1=link_sums[:, 1, 0:FEATURES], op=ALU.add
+                out=update[:], in0=bf_bf[:, 0:FEATURES], scalar=sums[:, L_M : L_M + 1],
+                in1=sum_tiles[batch][:, 0:FEATURES], op0=ALU.mult, op1=ALU.add,
             )
             update_tiles[batch] = (update, factor)
 
@@ -330,10 +318,12 @@ def tile_embed_update_pa_t_kernel(
             if in_range(i - 3):
                 transpose_h(i - 3)
                 relu_and_group_h(i - 3)
+            if in_range(i - 6):
+                add_link(i - 6, 0)
             if in_range(i - 4):
                 quantise_h(i - 4)
             if in_range(i - 6):
-                add_links(i - 6)
+                add_link(i - 6, 1)
             if ends_batch(i - 6):
                 finish_update((i - 6) // ROUNDS_PER_BATCH)
             if ends_batch(i - 7):

@@ -17,6 +17,7 @@ P = 128
 BATCHES, LINKS, IN, HID, CHANNELS = 4, 16, 1024, 512, 128
 FEATURES = CHANNELS - 1
 K_PASS = 4 * P
+PASS_WORDS = K_PASS // 2
 IN_PASSES = IN // K_PASS
 LN_EPS = 1e-5
 LINK_EPS = 1e-8
@@ -25,7 +26,13 @@ ROUND_TILES = 2
 ROUNDS = BATCHES * LINKS // ROUND_TILES
 ROUNDS_PER_BATCH = LINKS // ROUND_TILES
 LOADS_AHEAD = 6
-LAST_LAG = 8
+
+LAG_FIRST_MATMUL = 1
+LAG_TRANSPOSE_H = 3
+LAG_SECOND_MATMUL = 4
+LAG_ADD_LINKS = 6
+LAG_STATISTICS = 7
+LAG_NORM = 8
 
 FLOPS = 2 * BATCHES * P * LINKS * (IN * HID + HID * CHANNELS)
 
@@ -41,10 +48,17 @@ def tile_embed_update_pa_t_kernel(
         stage = ctx.enter_context(tc.tile_pool(name="stage", bufs=2))
         rows_pool = ctx.enter_context(tc.tile_pool(name="rows", bufs=3 * ROUND_TILES))
         finish_pool = ctx.enter_context(tc.tile_pool(name="finish", bufs=2))
-        xt_pool = ctx.enter_context(tc.psum_pool(name="xt", bufs=2))
-        acc_pool = ctx.enter_context(tc.psum_pool(name="acc", bufs=3))
+        xt_pool = ctx.enter_context(tc.psum_pool(name="xt", bufs=ROUND_TILES))
+        acc_pool = ctx.enter_context(tc.psum_pool(name="acc", bufs=ROUND_TILES + 1))
         ht_pool = ctx.enter_context(tc.psum_pool(name="ht", bufs=1))
         o_pool = ctx.enter_context(tc.psum_pool(name="o", bufs=2))
+
+        identity = const.tile([P, P], F32)
+        make_identity(nc, identity[:])
+        minus_half = const.tile([P, 1], F32)
+        nc.gpsimd.memset(minus_half[:], -0.5)
+        table_warmer = const.tile([P, 1], F32)
+        nc.scalar.activation(out=table_warmer[:], in_=minus_half[:], func=ACT.Sigmoid)
 
         x_tiles = {}
 
@@ -56,24 +70,15 @@ def tile_embed_update_pa_t_kernel(
             )
             x_tiles[r] = x_rows
 
-        identity = const.tile([P, P], F32)
-        make_identity(nc, identity[:])
-        minus_half = const.tile([P, 1], F32)
-        nc.gpsimd.memset(minus_half[:], -0.5)
-        minus_one = const.tile([P, 1], F32)
-        nc.gpsimd.memset(minus_one[:], -1.0)
-        table_warmer = const.tile([P, 1], F32)
-        nc.scalar.activation(out=table_warmer[:], in_=minus_half[:], func=ACT.Sigmoid)
-
         w1_scales = const.tile([P, IN_PASSES, HID], U8, align_bytes=64)
         wf_scales = const.tile([P, CHANNELS], U8, align_bytes=64)
         nc.vector.memset(w1_scales[:].rearrange("p g n -> p (g n)").bitcast(I32), 0)
         nc.vector.memset(wf_scales[:].bitcast(I32), 0)
 
-        def load_scales(plane, scale_rows):
+        def load_scales(scale_tile, scale_rows):
             for quadrant in range(4):
                 nc.sync.dma_start(
-                    out=plane[32 * quadrant : 32 * quadrant + 4].bitcast(I32),
+                    out=scale_tile[32 * quadrant : 32 * quadrant + 4].bitcast(I32),
                     in_=scale_rows[4 * quadrant : 4 * quadrant + 4].bitcast(I32),
                 )
 
@@ -112,7 +117,7 @@ def tile_embed_update_pa_t_kernel(
         L, L_M, L_G = 0, 1, 2
         terms = const.tile([P, 3, BATCHES * LINKS], F32)
 
-        xt_tiles, xq_tiles, acc_tiles, h_rows_tiles = {}, {}, {}, {}
+        xt_tiles, xg_tiles, xq_tiles, acc_tiles, h_rows_tiles = {}, {}, {}, {}, {}
         ht_tiles, hg_tiles, hq_tiles, o_tiles, sum_tiles = {}, {}, {}, {}, {}
 
         def transpose_x(r):
@@ -121,9 +126,10 @@ def tile_embed_update_pa_t_kernel(
                 x_t = xt_pool.tile([P, 2 * IN_PASSES, P], F32)
                 for g in range(IN_PASSES):
                     for u in range(2):
-                        first = g * (K_PASS // 2) + u
                         nc.tensor.transpose(
-                            x_t[:, 2 * g + u, :], words[:, first : (g + 1) * (K_PASS // 2) : 2], identity[:]
+                            x_t[:, 2 * g + u, :],
+                            words[:, g * PASS_WORDS + u : (g + 1) * PASS_WORDS : 2],
+                            identity[:],
                         )
                 xt_tiles[r, i] = x_t
 
@@ -134,15 +140,15 @@ def tile_embed_update_pa_t_kernel(
                     out=x_grouped[:, i].bitcast(F32),
                     in_=xt_tiles[r, i][:].rearrange("p (g u) t -> p g t u", u=2),
                 )
-            return x_grouped
+            xg_tiles[r] = x_grouped
 
-        def quantise_x(r, x_grouped):
+        def quantise_x(r):
             x_codes = stage.tile([P, ROUND_TILES, IN_PASSES, P], U32, align_bytes=64)
             x_scales = stage.tile([P, ROUND_TILES, IN_PASSES, P], U8, align_bytes=64)
             nc.vector.quantize_mx(
                 out=x_codes[:].rearrange("p i g t -> p (i g t)").bitcast(FP8X4),
                 scales=x_scales[:].rearrange("p i g t -> p (i g t)"),
-                in_=x_grouped[:].rearrange("p i g t j -> p (i g t j)"),
+                in_=xg_tiles[r][:].rearrange("p i g t j -> p (i g t j)"),
             )
             xq_tiles[r] = (x_codes, x_scales)
 
@@ -224,13 +230,19 @@ def tile_embed_update_pa_t_kernel(
                 func=ACT.Sigmoid,
                 bias=bf_bf[:, FEATURES:CHANNELS],
             )
-            nc.gpsimd.tensor_tensor(out=g_link[:, cols], in0=sigmoid[:, cols], in1=m_link[:, cols], op=ALU.mult)
+            nc.gpsimd.tensor_tensor(
+                out=g_link[:, cols], in0=sigmoid[:, cols], in1=m_link[:, cols], op=ALU.mult
+            )
             nc.gpsimd.tensor_scalar(
                 out=terms[:, L, cols], in0=g_link[:, cols], scalar1=LINK_EPS, scalar2=1.0,
                 op0=ALU.add, op1=ALU.mult,
             )
-            nc.gpsimd.tensor_tensor(out=terms[:, L_M, cols], in0=terms[:, L, cols], in1=m_link[:, cols], op=ALU.mult)
-            nc.gpsimd.tensor_tensor(out=terms[:, L_G, cols], in0=terms[:, L, cols], in1=g_link[:, cols], op=ALU.mult)
+            nc.gpsimd.tensor_tensor(
+                out=terms[:, L_M, cols], in0=terms[:, L, cols], in1=m_link[:, cols], op=ALU.mult
+            )
+            nc.gpsimd.tensor_tensor(
+                out=terms[:, L_G, cols], in0=terms[:, L, cols], in1=g_link[:, cols], op=ALU.mult
+            )
 
         def add_link(r, i):
             batch, link = divmod(r * ROUND_TILES + i, LINKS)
@@ -255,9 +267,9 @@ def tile_embed_update_pa_t_kernel(
                 out=sums[:], in_=terms[:, :, batch * LINKS : (batch + 1) * LINKS], axis=AXIS.X, op=ALU.add
             )
             inv_l = finish_pool.tile([P, 1], F32)
-            nc.gpsimd.tensor_tensor(out=inv_l[:], in0=sums[:, L : L + 1], in1=minus_one[:], op=ALU.pow)
+            nc.vector.reciprocal(out=inv_l[:], in_=sums[:, L : L + 1])
             factor = finish_pool.tile([P, 1], F32)
-            nc.gpsimd.tensor_scalar(
+            nc.vector.tensor_scalar(
                 out=factor[:], in0=sums[:, L_G : L_G + 1], scalar1=inv_l[:], scalar2=inv_l[:],
                 op0=ALU.mult, op1=ALU.mult,
             )
@@ -280,8 +292,8 @@ def tile_embed_update_pa_t_kernel(
             mean_var = finish_pool.tile([P, 2], F32)
             nc.vector.bn_aggr(out=mean_var[:], in_=stats[:])
             var_eps = finish_pool.tile([P, 1], F32)
-            nc.gpsimd.tensor_scalar(
-                out=var_eps[:], in0=mean_var[:, 1:2], scalar1=LN_EPS, scalar2=1.0, op0=ALU.add, op1=ALU.mult
+            nc.vector.tensor_scalar(
+                out=var_eps[:], in0=mean_var[:, 1:2], scalar1=LN_EPS, scalar2=None, op0=ALU.add
             )
             inv_std = finish_pool.tile([P, 1], F32)
             nc.gpsimd.tensor_tensor(out=inv_std[:], in0=var_eps[:], in1=minus_half[:], op=ALU.pow)
@@ -308,33 +320,32 @@ def tile_embed_update_pa_t_kernel(
         def ends_batch(r):
             return in_range(r) and r % ROUNDS_PER_BATCH == ROUNDS_PER_BATCH - 1
 
-        for i in range(ROUNDS + LAST_LAG):
-            x_grouped = None
+        for i in range(ROUNDS + LAG_NORM):
             if in_range(i):
                 transpose_x(i)
-                x_grouped = group_x(i)
+                group_x(i)
             if in_range(i + LOADS_AHEAD):
                 load_x(i + LOADS_AHEAD)
-            if in_range(i - 3):
-                transpose_h(i - 3)
-                relu_and_group_h(i - 3)
-            if in_range(i - 6):
-                add_link(i - 6, 0)
-            if in_range(i - 4):
-                quantise_h(i - 4)
-            if in_range(i - 6):
-                add_link(i - 6, 1)
-            if ends_batch(i - 6):
-                finish_update((i - 6) // ROUNDS_PER_BATCH)
-            if ends_batch(i - 7):
-                finish_statistics((i - 7) // ROUNDS_PER_BATCH)
-            if ends_batch(i - LAST_LAG):
-                finish_norm((i - LAST_LAG) // ROUNDS_PER_BATCH)
+            if in_range(i - LAG_TRANSPOSE_H):
+                transpose_h(i - LAG_TRANSPOSE_H)
+                relu_and_group_h(i - LAG_TRANSPOSE_H)
+            if in_range(i - LAG_ADD_LINKS):
+                add_link(i - LAG_ADD_LINKS, 0)
+            if in_range(i - LAG_SECOND_MATMUL):
+                quantise_h(i - LAG_SECOND_MATMUL)
+            if in_range(i - LAG_ADD_LINKS):
+                add_link(i - LAG_ADD_LINKS, 1)
+            if ends_batch(i - LAG_ADD_LINKS):
+                finish_update((i - LAG_ADD_LINKS) // ROUNDS_PER_BATCH)
+            if ends_batch(i - LAG_STATISTICS):
+                finish_statistics((i - LAG_STATISTICS) // ROUNDS_PER_BATCH)
+            if ends_batch(i - LAG_NORM):
+                finish_norm((i - LAG_NORM) // ROUNDS_PER_BATCH)
             if in_range(i):
-                quantise_x(i, x_grouped)
-            if in_range(i - 1):
-                first_matmul(i - 1)
-                add_bias(i - 1)
-            if in_range(i - 4):
-                second_matmul(i - 4)
-                gate(i - 4)
+                quantise_x(i)
+            if in_range(i - LAG_FIRST_MATMUL):
+                first_matmul(i - LAG_FIRST_MATMUL)
+                add_bias(i - LAG_FIRST_MATMUL)
+            if in_range(i - LAG_SECOND_MATMUL):
+                second_matmul(i - LAG_SECOND_MATMUL)
+                gate(i - LAG_SECOND_MATMUL)

@@ -57,6 +57,8 @@ def tile_embed_update_pa_t_kernel(
         make_identity(nc, identity[:])
         minus_half = const.tile([P, 1], F32)
         nc.gpsimd.memset(minus_half[:], -0.5)
+        minus_one = const.tile([P, 1], F32)
+        nc.gpsimd.memset(minus_one[:], -1.0)
         table_warmer = const.tile([P, 1], F32)
         nc.scalar.activation(out=table_warmer[:], in_=minus_half[:], func=ACT.Sigmoid)
 
@@ -145,11 +147,12 @@ def tile_embed_update_pa_t_kernel(
         def quantise_x(r):
             x_codes = stage.tile([P, ROUND_TILES, IN_PASSES, P], U32, align_bytes=64)
             x_scales = stage.tile([P, ROUND_TILES, IN_PASSES, P], U8, align_bytes=64)
-            nc.vector.quantize_mx(
-                out=x_codes[:].rearrange("p i g t -> p (i g t)").bitcast(FP8X4),
-                scales=x_scales[:].rearrange("p i g t -> p (i g t)"),
-                in_=xg_tiles[r][:].rearrange("p i g t j -> p (i g t j)"),
-            )
+            for i in range(ROUND_TILES):
+                nc.vector.quantize_mx(
+                    out=x_codes[:, i].rearrange("p g t -> p (g t)").bitcast(FP8X4),
+                    scales=x_scales[:, i].rearrange("p g t -> p (g t)"),
+                    in_=xg_tiles[r][:, i].rearrange("p g t j -> p (g t j)"),
+                )
             xq_tiles[r] = (x_codes, x_scales)
 
         def first_matmul(r):
@@ -267,9 +270,9 @@ def tile_embed_update_pa_t_kernel(
                 out=sums[:], in_=terms[:, :, batch * LINKS : (batch + 1) * LINKS], axis=AXIS.X, op=ALU.add
             )
             inv_l = finish_pool.tile([P, 1], F32)
-            nc.vector.reciprocal(out=inv_l[:], in_=sums[:, L : L + 1])
+            nc.gpsimd.tensor_tensor(out=inv_l[:], in0=sums[:, L : L + 1], in1=minus_one[:], op=ALU.pow)
             factor = finish_pool.tile([P, 1], F32)
-            nc.vector.tensor_scalar(
+            nc.gpsimd.tensor_scalar(
                 out=factor[:], in0=sums[:, L_G : L_G + 1], scalar1=inv_l[:], scalar2=inv_l[:],
                 op0=ALU.mult, op1=ALU.mult,
             )
@@ -292,8 +295,8 @@ def tile_embed_update_pa_t_kernel(
             mean_var = finish_pool.tile([P, 2], F32)
             nc.vector.bn_aggr(out=mean_var[:], in_=stats[:])
             var_eps = finish_pool.tile([P, 1], F32)
-            nc.vector.tensor_scalar(
-                out=var_eps[:], in0=mean_var[:, 1:2], scalar1=LN_EPS, scalar2=None, op0=ALU.add
+            nc.gpsimd.tensor_scalar(
+                out=var_eps[:], in0=mean_var[:, 1:2], scalar1=LN_EPS, scalar2=1.0, op0=ALU.add, op1=ALU.mult
             )
             inv_std = finish_pool.tile([P, 1], F32)
             nc.gpsimd.tensor_tensor(out=inv_std[:], in0=var_eps[:], in1=minus_half[:], op=ALU.pow)

@@ -16,23 +16,19 @@ AXIS = mybir.AxisListType
 P = 128
 BATCHES, LINKS, IN, HID, CHANNELS = 4, 16, 1024, 512, 128
 FEATURES = CHANNELS - 1
-K_PASS = 4 * P
+PACK = 4
+K_PASS = PACK * P
 PASS_WORDS = K_PASS // 2
 IN_PASSES = IN // K_PASS
 LN_EPS = 1e-5
 LINK_EPS = 1e-8
 
-ROUND_TILES = 2
-ROUNDS = BATCHES * LINKS // ROUND_TILES
-ROUNDS_PER_BATCH = LINKS // ROUND_TILES
-LOADS_AHEAD = 6
-
-LAG_FIRST_MATMUL = 1
-LAG_TRANSPOSE_H = 3
-LAG_SECOND_MATMUL = 4
-LAG_ADD_LINKS = 6
-LAG_STATISTICS = 7
-LAG_NORM = 8
+GROUP_TILES = 4
+GROUP_ROWS = GROUP_TILES * P
+GROUPS = BATCHES * LINKS // GROUP_TILES
+GROUPS_PER_BATCH = LINKS // GROUP_TILES
+PAIRS = GROUP_TILES // 2
+X_BUFS = 8
 
 FLOPS = 2 * BATCHES * P * LINKS * (IN * HID + HID * CHANNELS)
 
@@ -44,14 +40,10 @@ def tile_embed_update_pa_t_kernel(
     with ExitStack() as ctx:
         ctx.enter_context(tc.manual_schedule())
         const = ctx.enter_context(tc.tile_pool(name="const", bufs=1))
-        x_pool = ctx.enter_context(tc.tile_pool(name="x", bufs=LOADS_AHEAD))
+        x_pool = ctx.enter_context(tc.tile_pool(name="x", bufs=X_BUFS))
         stage = ctx.enter_context(tc.tile_pool(name="stage", bufs=2))
-        rows_pool = ctx.enter_context(tc.tile_pool(name="rows", bufs=3 * ROUND_TILES))
         finish_pool = ctx.enter_context(tc.tile_pool(name="finish", bufs=2))
-        xt_pool = ctx.enter_context(tc.psum_pool(name="xt", bufs=ROUND_TILES))
-        acc_pool = ctx.enter_context(tc.psum_pool(name="acc", bufs=ROUND_TILES + 1))
-        ht_pool = ctx.enter_context(tc.psum_pool(name="ht", bufs=1))
-        o_pool = ctx.enter_context(tc.psum_pool(name="o", bufs=2))
+        psum = ctx.enter_context(tc.psum_pool(name="psum", bufs=8))
 
         identity = const.tile([P, P], F32)
         make_identity(nc, identity[:])
@@ -64,17 +56,21 @@ def tile_embed_update_pa_t_kernel(
 
         x_tiles = {}
 
-        def load_x(r):
-            batch, first_link = divmod(r * ROUND_TILES, LINKS)
-            x_rows = x_pool.tile([P, ROUND_TILES, IN], BF16)
-            nc.sync.dma_start(
-                out=x_rows[:], in_=net_in[batch, :, first_link : first_link + ROUND_TILES, :]
-            )
-            x_tiles[r] = x_rows
+        def load_x(s, pieces):
+            batch, quarter = divmod(s, GROUPS_PER_BATCH)
+            first_link = quarter * GROUP_TILES
+            x_rows = x_pool.tile([P, GROUP_TILES, IN], BF16)
+            step = GROUP_TILES // pieces
+            for h in range(pieces):
+                nc.sync.dma_start(
+                    out=x_rows[:, h * step : (h + 1) * step, :],
+                    in_=net_in[batch, :, first_link + h * step : first_link + (h + 1) * step, :],
+                )
+            x_tiles[s] = x_rows
 
-        w1_scales = const.tile([P, IN_PASSES, HID], U8, align_bytes=64)
+        w1_scales_raw = const.tile([P, IN_PASSES, HID], U8, align_bytes=64)
         wf_scales = const.tile([P, CHANNELS], U8, align_bytes=64)
-        nc.vector.memset(w1_scales[:].rearrange("p g n -> p (g n)").bitcast(I32), 0)
+        nc.vector.memset(w1_scales_raw[:].rearrange("p g n -> p (g n)").bitcast(I32), 0)
         nc.vector.memset(wf_scales[:].bitcast(I32), 0)
 
         def load_scales(scale_tile, scale_rows):
@@ -84,34 +80,48 @@ def tile_embed_update_pa_t_kernel(
                     in_=scale_rows[4 * quadrant : 4 * quadrant + 4].bitcast(I32),
                 )
 
-        load_x(0)
-        load_scales(w1_scales, W1_scales.rearrange("g r n -> r g n"))
-        load_x(1)
-        w1_words = const.tile([P, IN_PASSES, 4 * HID], U8, align_bytes=64)
+        load_x(0, PAIRS)
+        load_scales(w1_scales_raw, W1_scales.rearrange("g r n -> r g n"))
+        w1_raw = const.tile([P, IN_PASSES, HID], I32, align_bytes=64)
         nc.sync.dma_start(
-            out=w1_words[:].bitcast(I32), in_=W1_words.rearrange("g p n t -> p g (n t)").bitcast(I32)
+            out=w1_raw[:], in_=W1_words.rearrange("g p n t -> p g (n t)").bitcast(I32)
         )
-        b1_bf = const.tile([P, HID], BF16)
-        nc.sync.dma_start(out=b1_bf[:], in_=b1.partition_broadcast(P))
-        load_x(2)
+        b1_bf = const.tile([P, PACK], BF16)
+        nc.sync.dma_start(out=b1_bf[:], in_=b1.rearrange("(p t) -> p t", t=PACK))
+        load_x(1, PAIRS)
         wf_words = const.tile([P, 4 * CHANNELS], U8, align_bytes=64)
         nc.sync.dma_start(
             out=wf_words[:].bitcast(I32), in_=Wf_words[0].rearrange("p n t -> p (n t)").bitcast(I32)
         )
         load_scales(wf_scales, Wf_scales[0])
-        load_x(3)
+        load_x(2, 1)
         bf_bf = const.tile([P, CHANNELS], BF16)
         nc.sync.dma_start(out=bf_bf[:], in_=b_f.partition_broadcast(P))
         m_bf = const.tile([P, BATCHES, LINKS], BF16)
         nc.sync.dma_start(out=m_bf[:], in_=m.rearrange("b s k o -> s b (k o)"))
-        for r in range(4, LOADS_AHEAD):
-            load_x(r)
+        load_x(3, 1)
+        load_x(4, 1)
         gamma_bf = const.tile([P, FEATURES], BF16)
         nc.sync.dma_start(out=gamma_bf[:], in_=gamma.partition_broadcast(P))
         beta_bf = const.tile([P, FEATURES], BF16)
         nc.sync.dma_start(out=beta_bf[:], in_=beta.partition_broadcast(P))
         embeds_bf = const.tile([P, BATCHES, FEATURES], BF16)
         nc.sync.dma_start(out=embeds_bf[:], in_=embeds.rearrange("b s c -> s b c"))
+        for s in range(5, X_BUFS):
+            load_x(s, 1)
+
+        w1_words = const.tile([P, IN_PASSES, PACK, P], I32, align_bytes=64)
+        w1_scales = const.tile([P, IN_PASSES, PACK, P], U8, align_bytes=64)
+
+        def reorder_w1():
+            for g in range(IN_PASSES):
+                nc.vector.tensor_copy(
+                    out=w1_scales[:, g], in_=w1_scales_raw[:, g, :].rearrange("p (c t) -> p t c", t=PACK)
+                )
+            for g in range(IN_PASSES):
+                nc.vector.tensor_copy(
+                    out=w1_words[:, g], in_=w1_raw[:, g, :].rearrange("p (c t) -> p t c", t=PACK)
+                )
 
         m_link = m_bf[:].rearrange("s b k -> s (b k)")
         sigmoid = const.tile([P, BATCHES * LINKS], F32)
@@ -119,117 +129,100 @@ def tile_embed_update_pa_t_kernel(
         L, L_M, L_G = 0, 1, 2
         terms = const.tile([P, 3, BATCHES * LINKS], F32)
 
-        xt_tiles, xg_tiles, xq_tiles, acc_tiles, h_rows_tiles = {}, {}, {}, {}, {}
-        ht_tiles, hg_tiles, hq_tiles, o_tiles, sum_tiles = {}, {}, {}, {}, {}
+        xt_tiles, xg_tiles, xq_tiles, acc_tiles, hf_tiles = {}, {}, {}, {}, {}
+        hg_tiles, hq_tiles, o_tiles, sum_tiles = {}, {}, {}, {}
+        BANKS = [(pair, g) for pair in range(PAIRS) for g in range(IN_PASSES)]
 
-        def transpose_x(r):
-            for i in range(ROUND_TILES):
-                words = x_tiles[r][:, i, :].bitcast(F32)
-                x_t = xt_pool.tile([P, 2 * IN_PASSES, P], F32)
-                for g in range(IN_PASSES):
+        def transpose_x(s):
+            for pair, g in BANKS:
+                x_t = psum.tile([P, 2, 2, P], F32, tag="bank")
+                for j in range(2):
+                    words = x_tiles[s][:, 2 * pair + j, :].bitcast(F32)
                     for u in range(2):
                         nc.tensor.transpose(
-                            x_t[:, 2 * g + u, :],
+                            x_t[:, j, u, :],
                             words[:, g * PASS_WORDS + u : (g + 1) * PASS_WORDS : 2],
                             identity[:],
                         )
-                xt_tiles[r, i] = x_t
+                xt_tiles[s, pair, g] = x_t
 
-        def group_x(r):
-            x_grouped = stage.tile([P, ROUND_TILES, IN_PASSES, P, 4], BF16, align_bytes=64)
-            for i in range(ROUND_TILES):
+        def group_x(s):
+            x_grouped = stage.tile([P, IN_PASSES, GROUP_TILES, P, PACK], BF16, align_bytes=64)
+            for pair, g in BANKS:
                 nc.scalar.copy(
-                    out=x_grouped[:, i].bitcast(F32),
-                    in_=xt_tiles[r, i][:].rearrange("p (g u) t -> p g t u", u=2),
+                    out=x_grouped[:, g, 2 * pair : 2 * pair + 2].bitcast(F32),
+                    in_=xt_tiles[s, pair, g][:].rearrange("p j u t -> p j t u"),
                 )
-            xg_tiles[r] = x_grouped
+            xg_tiles[s] = x_grouped
+            x_codes = stage.tile([P, IN_PASSES, GROUP_TILES, P], U32, align_bytes=64)
+            x_scales = stage.tile([P, IN_PASSES, GROUP_TILES, P], U8, align_bytes=64)
+            xq_tiles[s] = (x_codes, x_scales)
 
-        def quantise_x(r):
-            x_codes = stage.tile([P, ROUND_TILES, IN_PASSES, P], U32, align_bytes=64)
-            x_scales = stage.tile([P, ROUND_TILES, IN_PASSES, P], U8, align_bytes=64)
-            for i in range(ROUND_TILES):
-                nc.vector.quantize_mx(
-                    out=x_codes[:, i].rearrange("p g t -> p (g t)").bitcast(FP8X4),
-                    scales=x_scales[:, i].rearrange("p g t -> p (g t)"),
-                    in_=xg_tiles[r][:, i].rearrange("p g t j -> p (g t j)"),
-                )
-            xq_tiles[r] = (x_codes, x_scales)
+        def quantise_x(s, bank):
+            pair, g = BANKS[bank]
+            x_codes, x_scales = xq_tiles[s]
+            tiles = slice(2 * pair, 2 * pair + 2)
+            nc.vector.quantize_mx(
+                out=x_codes[:, g, tiles].rearrange("p j t -> p (j t)").bitcast(FP8X4),
+                scales=x_scales[:, g, tiles].rearrange("p j t -> p (j t)"),
+                in_=xg_tiles[s][:, g, tiles].rearrange("p j t e -> p (j t e)"),
+            )
 
-        def first_matmul(r):
-            x_codes, x_scales = xq_tiles[r]
-            for i in range(ROUND_TILES):
-                acc = acc_pool.tile([P, HID], F32)
+        def first_matmul(s):
+            x_codes, x_scales = xq_tiles[s]
+            h_flat = stage.tile([P, PACK, GROUP_ROWS], BF16)
+            for t in range(PACK):
+                acc = psum.tile([P, GROUP_ROWS], F32, tag="bank")
                 for g in range(IN_PASSES):
                     nc.tensor.matmul_mx(
                         out=acc[:],
-                        lhsT=x_codes[:, i, g, :].bitcast(FP8X4),
-                        lhsT_scale=x_scales[:, i, g, :],
-                        rhs=w1_words[:, g, :].bitcast(FP8X4),
-                        rhs_scale=w1_scales[:, g, :],
+                        lhsT=w1_words[:, g, t, :].bitcast(FP8X4),
+                        lhsT_scale=w1_scales[:, g, t, :],
+                        rhs=x_codes[:, g].rearrange("p j t -> p (j t)").bitcast(FP8X4),
+                        rhs_scale=x_scales[:, g].rearrange("p j t -> p (j t)"),
                         start=(g == 0),
                         stop=(g == IN_PASSES - 1),
                     )
-                acc_tiles[r, i] = acc
-
-        def add_bias(r):
-            for i in range(ROUND_TILES):
-                h_rows = rows_pool.tile([P, HID], BF16)
-                nc.vector.tensor_tensor(
-                    out=h_rows[:].rearrange("t (u q e) -> t u q e", u=2, e=2),
-                    in0=acc_tiles[r, i][:].rearrange("t (q u e) -> t u q e", u=2, e=2),
-                    in1=b1_bf[:].rearrange("t (q u e) -> t u q e", u=2, e=2),
-                    op=ALU.add,
-                )
-                h_rows_tiles[r, i] = h_rows
-
-        def transpose_h(r):
-            h_t = ht_pool.tile([P, ROUND_TILES, 2, P], F32)
-            for i in range(ROUND_TILES):
-                words = h_rows_tiles[r, i][:].bitcast(F32)
-                for u in range(2):
-                    nc.tensor.transpose(h_t[:, i, u, :], words[:, u * P : (u + 1) * P], identity[:])
-            ht_tiles[r] = h_t
-
-        def relu_and_group_h(r):
-            h_grouped = stage.tile([P, ROUND_TILES, P, 4], BF16, align_bytes=64)
-            for i in range(ROUND_TILES):
                 nc.scalar.activation(
-                    out=h_grouped[:, i].rearrange("p t (u e) -> p t u e", u=2),
-                    in_=ht_tiles[r][:, i].bitcast(BF16).rearrange("p u (t e) -> p t u e", e=2),
-                    func=ACT.Relu,
+                    out=h_flat[:, t, :], in_=acc[:], func=ACT.Relu, bias=b1_bf[:, t : t + 1]
                 )
-            hg_tiles[r] = h_grouped
+            hf_tiles[s] = h_flat
 
-        def quantise_h(r):
-            h_codes = stage.tile([P, ROUND_TILES, P], U32, align_bytes=64)
-            h_scales = stage.tile([P, ROUND_TILES, P], U8, align_bytes=64)
+        def interleave_h(s):
+            h_grouped = stage.tile([P, GROUP_ROWS, PACK], BF16, align_bytes=64)
+            nc.vector.tensor_copy(out=h_grouped[:], in_=hf_tiles[s][:].rearrange("p t n -> p n t"))
+            hg_tiles[s] = h_grouped
+
+        def quantise_h(s):
+            h_codes = stage.tile([P, GROUP_TILES, P], U32, align_bytes=64)
+            h_scales = stage.tile([P, GROUP_TILES, P], U8, align_bytes=64)
             nc.vector.quantize_mx(
-                out=h_codes[:].rearrange("p i t -> p (i t)").bitcast(FP8X4),
-                scales=h_scales[:].rearrange("p i t -> p (i t)"),
-                in_=hg_tiles[r][:].rearrange("p i t j -> p (i t j)"),
+                out=h_codes[:].rearrange("p j t -> p (j t)").bitcast(FP8X4),
+                scales=h_scales[:].rearrange("p j t -> p (j t)"),
+                in_=hg_tiles[s][:].rearrange("p n t -> p (n t)"),
             )
-            hq_tiles[r] = (h_codes, h_scales)
+            hq_tiles[s] = (h_codes, h_scales)
 
-        def second_matmul(r):
-            h_codes, h_scales = hq_tiles[r]
-            o = o_pool.tile([P, ROUND_TILES, CHANNELS], F32)
-            for i in range(ROUND_TILES):
+        def second_matmul(s):
+            h_codes, h_scales = hq_tiles[s]
+            o = psum.tile([P, GROUP_TILES, CHANNELS], F32, tag="bank")
+            for j in range(GROUP_TILES):
                 nc.tensor.matmul_mx(
-                    out=o[:, i, :],
-                    lhsT=h_codes[:, i, :].bitcast(FP8X4),
-                    lhsT_scale=h_scales[:, i, :],
+                    out=o[:, j, :],
+                    lhsT=h_codes[:, j, :].bitcast(FP8X4),
+                    lhsT_scale=h_scales[:, j, :],
                     rhs=wf_words[:].bitcast(FP8X4),
                     rhs_scale=wf_scales[:],
                     start=True,
                     stop=True,
                 )
-            o_tiles[r] = o
+            o_tiles[s] = o
 
-        def gate(r):
-            cols = slice(r * ROUND_TILES, (r + 1) * ROUND_TILES)
+        def gate(s):
+            cols = slice(s * GROUP_TILES, (s + 1) * GROUP_TILES)
             nc.scalar.activation(
                 out=sigmoid[:, cols],
-                in_=o_tiles[r][:, :, FEATURES],
+                in_=o_tiles[s][:, :, FEATURES],
                 func=ACT.Sigmoid,
                 bias=bf_bf[:, FEATURES:CHANNELS],
             )
@@ -247,18 +240,18 @@ def tile_embed_update_pa_t_kernel(
                 out=terms[:, L_G, cols], in0=terms[:, L, cols], in1=g_link[:, cols], op=ALU.mult
             )
 
-        def add_link(r, i):
-            batch, link = divmod(r * ROUND_TILES + i, LINKS)
-            weight = terms[:, L_M, r * ROUND_TILES + i : r * ROUND_TILES + i + 1]
+        def add_link(s, j):
+            batch, link = divmod(s * GROUP_TILES + j, LINKS)
+            weight = terms[:, L_M, s * GROUP_TILES + j : s * GROUP_TILES + j + 1]
             if link == 0:
                 link_sum = finish_pool.tile([P, CHANNELS], F32)
                 nc.vector.tensor_scalar(
-                    out=link_sum[:], in0=o_tiles[r][:, i, :], scalar1=weight, scalar2=None, op0=ALU.mult
+                    out=link_sum[:], in0=o_tiles[s][:, j, :], scalar1=weight, scalar2=None, op0=ALU.mult
                 )
                 sum_tiles[batch] = link_sum
             else:
                 nc.vector.scalar_tensor_tensor(
-                    out=sum_tiles[batch][:], in0=o_tiles[r][:, i, :], scalar=weight,
+                    out=sum_tiles[batch][:], in0=o_tiles[s][:, j, :], scalar=weight,
                     in1=sum_tiles[batch][:], op0=ALU.mult, op1=ALU.add,
                 )
 
@@ -317,38 +310,38 @@ def tile_embed_update_pa_t_kernel(
             )
             nc.sync.dma_start(out=out[batch], in_=result[:])
 
-        def in_range(r):
-            return 0 <= r < ROUNDS
+        def in_range(s):
+            return 0 <= s < GROUPS
 
-        def ends_batch(r):
-            return in_range(r) and r % ROUNDS_PER_BATCH == ROUNDS_PER_BATCH - 1
+        def ends_batch(s):
+            return in_range(s) and s % GROUPS_PER_BATCH == GROUPS_PER_BATCH - 1
 
-        for i in range(ROUNDS + LAG_NORM):
+        for i in range(-1, GROUPS + 4):
+            if in_range(i - 2):
+                gate(i - 2)
+            if in_range(i + 1):
+                transpose_x(i + 1)
+                group_x(i + 1)
+            if i >= 0 and in_range(i + X_BUFS):
+                load_x(i + X_BUFS, 1)
+            if in_range(i - 1):
+                interleave_h(i - 1)
+            for bank in range(len(BANKS)):
+                if in_range(i - 2):
+                    add_link(i - 2, bank)
+                if in_range(i + 1):
+                    quantise_x(i + 1, bank)
+                if bank == 0 and in_range(i - 1):
+                    quantise_h(i - 1)
+            if i == -1:
+                reorder_w1()
+            if ends_batch(i - 2):
+                finish_update((i - 2) // GROUPS_PER_BATCH)
+            if ends_batch(i - 3):
+                finish_statistics((i - 3) // GROUPS_PER_BATCH)
+            if ends_batch(i - 4):
+                finish_norm((i - 4) // GROUPS_PER_BATCH)
             if in_range(i):
-                transpose_x(i)
-                group_x(i)
-            if in_range(i + LOADS_AHEAD):
-                load_x(i + LOADS_AHEAD)
-            if in_range(i - LAG_TRANSPOSE_H):
-                transpose_h(i - LAG_TRANSPOSE_H)
-                relu_and_group_h(i - LAG_TRANSPOSE_H)
-            if in_range(i - LAG_ADD_LINKS):
-                add_link(i - LAG_ADD_LINKS, 0)
-            if in_range(i - LAG_SECOND_MATMUL):
-                quantise_h(i - LAG_SECOND_MATMUL)
-            if in_range(i - LAG_ADD_LINKS):
-                add_link(i - LAG_ADD_LINKS, 1)
-            if ends_batch(i - LAG_ADD_LINKS):
-                finish_update((i - LAG_ADD_LINKS) // ROUNDS_PER_BATCH)
-            if ends_batch(i - LAG_STATISTICS):
-                finish_statistics((i - LAG_STATISTICS) // ROUNDS_PER_BATCH)
-            if ends_batch(i - LAG_NORM):
-                finish_norm((i - LAG_NORM) // ROUNDS_PER_BATCH)
-            if in_range(i):
-                quantise_x(i)
-            if in_range(i - LAG_FIRST_MATMUL):
-                first_matmul(i - LAG_FIRST_MATMUL)
-                add_bias(i - LAG_FIRST_MATMUL)
-            if in_range(i - LAG_SECOND_MATMUL):
-                second_matmul(i - LAG_SECOND_MATMUL)
-                gate(i - LAG_SECOND_MATMUL)
+                first_matmul(i)
+            if in_range(i - 1):
+                second_matmul(i - 1)

@@ -43,7 +43,8 @@ def tile_embed_update_pa_t_kernel(
         x_pool = ctx.enter_context(tc.tile_pool(name="x", bufs=X_BUFS))
         stage = ctx.enter_context(tc.tile_pool(name="stage", bufs=2))
         finish_pool = ctx.enter_context(tc.tile_pool(name="finish", bufs=2))
-        psum = ctx.enter_context(tc.psum_pool(name="psum", bufs=8))
+        psum = ctx.enter_context(tc.psum_pool(name="psum", bufs=6))
+        o_pool = ctx.enter_context(tc.psum_pool(name="o", bufs=2))
 
         identity = const.tile([P, P], F32)
         make_identity(nc, identity[:])
@@ -205,7 +206,7 @@ def tile_embed_update_pa_t_kernel(
 
         def second_matmul(s):
             h_codes, h_scales = hq_tiles[s]
-            o = psum.tile([P, GROUP_TILES, CHANNELS], F32, tag="bank")
+            o = o_pool.tile([P, GROUP_TILES, CHANNELS], F32)
             for j in range(GROUP_TILES):
                 nc.tensor.matmul_mx(
                     out=o[:, j, :],
@@ -226,15 +227,25 @@ def tile_embed_update_pa_t_kernel(
                 func=ACT.Sigmoid,
                 bias=bf_bf[:, FEATURES:CHANNELS],
             )
-            nc.gpsimd.tensor_tensor(
+
+        def link_gate(s):
+            cols = slice(s * GROUP_TILES, (s + 1) * GROUP_TILES)
+            nc.vector.tensor_tensor(
                 out=g_link[:, cols], in0=sigmoid[:, cols], in1=m_link[:, cols], op=ALU.mult
             )
+
+        def link_weight(s):
+            cols = slice(s * GROUP_TILES, (s + 1) * GROUP_TILES)
+            nc.vector.scalar_tensor_tensor(
+                out=terms[:, L_M, cols], in0=g_link[:, cols], scalar=LINK_EPS, in1=m_link[:, cols],
+                op0=ALU.add, op1=ALU.mult,
+            )
+
+        def batch_terms(batch):
+            cols = slice(batch * LINKS, (batch + 1) * LINKS)
             nc.gpsimd.tensor_scalar(
                 out=terms[:, L, cols], in0=g_link[:, cols], scalar1=LINK_EPS, scalar2=1.0,
                 op0=ALU.add, op1=ALU.mult,
-            )
-            nc.gpsimd.tensor_tensor(
-                out=terms[:, L_M, cols], in0=terms[:, L, cols], in1=m_link[:, cols], op=ALU.mult
             )
             nc.gpsimd.tensor_tensor(
                 out=terms[:, L_G, cols], in0=terms[:, L, cols], in1=g_link[:, cols], op=ALU.mult
@@ -316,32 +327,48 @@ def tile_embed_update_pa_t_kernel(
         def ends_batch(s):
             return in_range(s) and s % GROUPS_PER_BATCH == GROUPS_PER_BATCH - 1
 
-        for i in range(-1, GROUPS + 4):
-            if in_range(i - 2):
-                gate(i - 2)
+        for i in range(-1, GROUPS + 5):
             if in_range(i + 1):
                 transpose_x(i + 1)
                 group_x(i + 1)
             if i >= 0 and in_range(i + X_BUFS):
                 load_x(i + X_BUFS, 1)
+            if in_range(i - 2):
+                second_matmul(i - 2)
+                gate(i - 2)
+            if in_range(i - 3):
+                link_gate(i - 3)
+                if ends_batch(i - 3):
+                    batch_terms((i - 3) // GROUPS_PER_BATCH)
             if in_range(i - 1):
                 interleave_h(i - 1)
-            for bank in range(len(BANKS)):
-                if in_range(i - 2):
-                    add_link(i - 2, bank)
-                if in_range(i + 1):
-                    quantise_x(i + 1, bank)
-                if bank == 0 and in_range(i - 1):
-                    quantise_h(i - 1)
+            if in_range(i - 3):
+                link_weight(i - 3)
+            if in_range(i + 1):
+                quantise_x(i + 1, 0)
+            if in_range(i - 3):
+                add_link(i - 3, 0)
+            if in_range(i - 1):
+                quantise_h(i - 1)
+            if in_range(i - 3):
+                add_link(i - 3, 1)
+            if in_range(i + 1):
+                quantise_x(i + 1, 1)
+            if in_range(i - 3):
+                add_link(i - 3, 2)
+            if in_range(i + 1):
+                quantise_x(i + 1, 2)
+            if in_range(i - 3):
+                add_link(i - 3, 3)
+            if in_range(i + 1):
+                quantise_x(i + 1, 3)
             if i == -1:
                 reorder_w1()
-            if ends_batch(i - 2):
-                finish_update((i - 2) // GROUPS_PER_BATCH)
             if ends_batch(i - 3):
-                finish_statistics((i - 3) // GROUPS_PER_BATCH)
+                finish_update((i - 3) // GROUPS_PER_BATCH)
             if ends_batch(i - 4):
-                finish_norm((i - 4) // GROUPS_PER_BATCH)
+                finish_statistics((i - 4) // GROUPS_PER_BATCH)
+            if ends_batch(i - 5):
+                finish_norm((i - 5) // GROUPS_PER_BATCH)
             if in_range(i):
                 first_matmul(i)
-            if in_range(i - 1):
-                second_matmul(i - 1)

@@ -29,6 +29,10 @@ GROUPS = BATCHES * LINKS // GROUP_TILES
 GROUPS_PER_BATCH = LINKS // GROUP_TILES
 PAIRS = GROUP_TILES // 2
 X_BUFS = 8
+SPLIT_GROUPS = 2
+UNITS = [(s, 0, GROUP_TILES) for s in range(GROUPS - SPLIT_GROUPS)] + [
+    (s, j, GROUP_TILES // 2) for s in range(GROUPS - SPLIT_GROUPS, GROUPS) for j in (0, GROUP_TILES // 2)
+]
 
 FLOPS = 2 * BATCHES * P * LINKS * (IN * HID + HID * CHANNELS)
 
@@ -48,12 +52,10 @@ def tile_embed_update_pa_t_kernel(
 
         identity = const.tile([P, P], F32)
         make_identity(nc, identity[:])
-        minus_half = const.tile([P, 1], F32)
+        minus_half = const.tile([P, 2], F32)
         nc.gpsimd.memset(minus_half[:], -0.5)
-        minus_one = const.tile([P, 1], F32)
-        nc.gpsimd.memset(minus_one[:], -1.0)
         table_warmer = const.tile([P, 1], F32)
-        nc.scalar.activation(out=table_warmer[:], in_=minus_half[:], func=ACT.Sigmoid)
+        nc.scalar.activation(out=table_warmer[:], in_=minus_half[:, 0:1], func=ACT.Sigmoid)
 
         x_tiles = {}
 
@@ -127,11 +129,9 @@ def tile_embed_update_pa_t_kernel(
         m_link = m_bf[:].rearrange("s b k -> s (b k)")
         sigmoid = const.tile([P, BATCHES * LINKS], F32)
         g_link = const.tile([P, BATCHES * LINKS], F32)
-        L, L_M, L_G = 0, 1, 2
-        terms = const.tile([P, 3, BATCHES * LINKS], F32)
+        weight_link = const.tile([P, BATCHES * LINKS], F32)
 
-        xt_tiles, xg_tiles, xq_tiles, acc_tiles, hf_tiles = {}, {}, {}, {}, {}
-        hg_tiles, hq_tiles, o_tiles, sum_tiles = {}, {}, {}, {}
+        xt_tiles, xg_tiles, xq_tiles = {}, {}, {}
         BANKS = [(pair, g) for pair in range(PAIRS) for g in range(IN_PASSES)]
 
         def transpose_x(s):
@@ -169,45 +169,55 @@ def tile_embed_update_pa_t_kernel(
                 in_=xg_tiles[s][:, g, tiles].rearrange("p j t e -> p (j t e)"),
             )
 
-        def first_matmul(s):
+        hf_tiles, hg_tiles, hq_tiles, o_tiles, sum_tiles = {}, {}, {}, {}, {}
+
+        def columns(u):
+            s, first, tiles = UNITS[u]
+            return slice(s * GROUP_TILES + first, s * GROUP_TILES + first + tiles)
+
+        def first_matmul(u):
+            s, first, tiles = UNITS[u]
             x_codes, x_scales = xq_tiles[s]
-            h_flat = stage.tile([P, PACK, GROUP_ROWS], BF16)
+            h_flat = stage.tile([P, PACK, tiles * P], BF16)
             for t in range(PACK):
-                acc = psum.tile([P, GROUP_ROWS], F32, tag="bank")
+                acc = psum.tile([P, tiles * P], F32, tag="bank")
                 for g in range(IN_PASSES):
                     nc.tensor.matmul_mx(
                         out=acc[:],
                         lhsT=w1_words[:, g, t, :].bitcast(FP8X4),
                         lhsT_scale=w1_scales[:, g, t, :],
-                        rhs=x_codes[:, g].rearrange("p j t -> p (j t)").bitcast(FP8X4),
-                        rhs_scale=x_scales[:, g].rearrange("p j t -> p (j t)"),
+                        rhs=x_codes[:, g, first : first + tiles].rearrange("p j t -> p (j t)").bitcast(FP8X4),
+                        rhs_scale=x_scales[:, g, first : first + tiles].rearrange("p j t -> p (j t)"),
                         start=(g == 0),
                         stop=(g == IN_PASSES - 1),
                     )
                 nc.scalar.activation(
                     out=h_flat[:, t, :], in_=acc[:], func=ACT.Relu, bias=b1_bf[:, t : t + 1]
                 )
-            hf_tiles[s] = h_flat
+            hf_tiles[u] = h_flat
 
-        def interleave_h(s):
-            h_grouped = stage.tile([P, GROUP_ROWS, PACK], BF16, align_bytes=64)
-            nc.vector.tensor_copy(out=h_grouped[:], in_=hf_tiles[s][:].rearrange("p t n -> p n t"))
-            hg_tiles[s] = h_grouped
+        def interleave_h(u):
+            h_grouped = stage.tile([P, UNITS[u][2] * P, PACK], BF16, align_bytes=64)
+            nc.vector.tensor_copy(out=h_grouped[:], in_=hf_tiles[u][:].rearrange("p t n -> p n t"))
+            hg_tiles[u] = h_grouped
 
-        def quantise_h(s):
-            h_codes = stage.tile([P, GROUP_TILES, P], U32, align_bytes=64)
-            h_scales = stage.tile([P, GROUP_TILES, P], U8, align_bytes=64)
+        def quantise_h(u):
+            h_codes = stage.tile([P, UNITS[u][2], P], U32, align_bytes=64)
+            h_scales = stage.tile([P, UNITS[u][2], P], U8, align_bytes=64)
             nc.vector.quantize_mx(
                 out=h_codes[:].rearrange("p j t -> p (j t)").bitcast(FP8X4),
                 scales=h_scales[:].rearrange("p j t -> p (j t)"),
-                in_=hg_tiles[s][:].rearrange("p n t -> p (n t)"),
+                in_=hg_tiles[u][:].rearrange("p n t -> p (n t)"),
             )
-            hq_tiles[s] = (h_codes, h_scales)
+            hq_tiles[u] = (h_codes, h_scales)
 
-        def second_matmul(s):
-            h_codes, h_scales = hq_tiles[s]
-            o = o_pool.tile([P, GROUP_TILES, CHANNELS], F32)
-            for j in range(GROUP_TILES):
+        def second_matmul(u, from_ring=False):
+            h_codes, h_scales = hq_tiles[u]
+            if from_ring:
+                o = psum.tile([P, UNITS[u][2], CHANNELS], F32, tag="bank")
+            else:
+                o = o_pool.tile([P, UNITS[u][2], CHANNELS], F32)
+            for j in range(UNITS[u][2]):
                 nc.tensor.matmul_mx(
                     out=o[:, j, :],
                     lhsT=h_codes[:, j, :].bitcast(FP8X4),
@@ -217,158 +227,258 @@ def tile_embed_update_pa_t_kernel(
                     start=True,
                     stop=True,
                 )
-            o_tiles[s] = o
+            o_tiles[u] = o
 
-        def gate(s):
-            cols = slice(s * GROUP_TILES, (s + 1) * GROUP_TILES)
+        def gate(u):
             nc.scalar.activation(
-                out=sigmoid[:, cols],
-                in_=o_tiles[s][:, :, FEATURES],
+                out=sigmoid[:, columns(u)],
+                in_=o_tiles[u][:, :, FEATURES],
                 func=ACT.Sigmoid,
                 bias=bf_bf[:, FEATURES:CHANNELS],
             )
 
-        def link_gate(s):
-            cols = slice(s * GROUP_TILES, (s + 1) * GROUP_TILES)
+        def link_gate(cols):
             nc.vector.tensor_tensor(
                 out=g_link[:, cols], in0=sigmoid[:, cols], in1=m_link[:, cols], op=ALU.mult
             )
 
-        def link_weight(s):
-            cols = slice(s * GROUP_TILES, (s + 1) * GROUP_TILES)
+        def link_weight(cols):
             nc.vector.scalar_tensor_tensor(
-                out=terms[:, L_M, cols], in0=g_link[:, cols], scalar=LINK_EPS, in1=m_link[:, cols],
+                out=weight_link[:, cols], in0=g_link[:, cols], scalar=LINK_EPS, in1=m_link[:, cols],
                 op0=ALU.add, op1=ALU.mult,
             )
 
-        def batch_terms(batch):
-            cols = slice(batch * LINKS, (batch + 1) * LINKS)
-            nc.gpsimd.tensor_scalar(
-                out=terms[:, L, cols], in0=g_link[:, cols], scalar1=LINK_EPS, scalar2=1.0,
-                op0=ALU.add, op1=ALU.mult,
-            )
-            nc.gpsimd.tensor_tensor(
-                out=terms[:, L_G, cols], in0=terms[:, L, cols], in1=g_link[:, cols], op=ALU.mult
-            )
-
-        def add_link(s, j):
-            batch, link = divmod(s * GROUP_TILES + j, LINKS)
-            weight = terms[:, L_M, s * GROUP_TILES + j : s * GROUP_TILES + j + 1]
-            if link == 0:
-                link_sum = finish_pool.tile([P, CHANNELS], F32)
+        def add_link(u, j):
+            column = columns(u).start + j
+            batch, link = divmod(column, LINKS)
+            weight = weight_link[:, column : column + 1]
+            if link < 2:
+                link_sum = finish_pool.tile([P, CHANNELS], F32, tag="link_sum%d" % link)
                 nc.vector.tensor_scalar(
-                    out=link_sum[:], in0=o_tiles[s][:, j, :], scalar1=weight, scalar2=None, op0=ALU.mult
+                    out=link_sum[:], in0=o_tiles[u][:, j, :], scalar1=weight, scalar2=None, op0=ALU.mult
                 )
-                sum_tiles[batch] = link_sum
+                sum_tiles[batch, link] = link_sum
             else:
+                link_sum = sum_tiles[batch, link % 2]
                 nc.vector.scalar_tensor_tensor(
-                    out=sum_tiles[batch][:], in0=o_tiles[s][:, j, :], scalar=weight,
-                    in1=sum_tiles[batch][:], op0=ALU.mult, op1=ALU.add,
+                    out=link_sum[:], in0=o_tiles[u][:, j, :], scalar=weight, in1=link_sum[:],
+                    op0=ALU.mult, op1=ALU.add,
                 )
 
-        update_tiles, e_tiles, norm_tiles = {}, {}, {}
+        L, L_M, L_G = 0, 1, 2
+        sums_tiles, factor_tiles, e_tiles, norm_tiles = {}, {}, {}, {}
 
-        def finish_update(batch):
+        def finish_sums(batch):
+            cols = slice(batch * LINKS, (batch + 1) * LINKS)
             sums = finish_pool.tile([P, 3], F32)
-            nc.vector.tensor_reduce(
-                out=sums[:], in_=terms[:, :, batch * LINKS : (batch + 1) * LINKS], axis=AXIS.X, op=ALU.add
+            terms = finish_pool.tile([P, 2, LINKS], F32)
+            nc.vector.tensor_scalar(
+                out=terms[:, 0, :], in0=g_link[:, cols], scalar1=LINK_EPS, scalar2=None,
+                op0=ALU.add, op1=ALU.add, accum_out=sums[:, L : L + 1],
             )
+            nc.vector.scalar_tensor_tensor(
+                out=terms[:, 1, :], in0=g_link[:, cols], scalar=LINK_EPS, in1=g_link[:, cols],
+                op0=ALU.add, op1=ALU.mult, accum_out=sums[:, L_G : L_G + 1],
+            )
+            sums_tiles[batch] = sums
+
+        def finish_sum_weights(batch):
+            nc.vector.tensor_reduce(
+                out=sums_tiles[batch][:, L_M : L_M + 1],
+                in_=weight_link[:, batch * LINKS : (batch + 1) * LINKS], axis=AXIS.X, op=ALU.add,
+            )
+
+        def finish_invert(batch):
             inv_l = finish_pool.tile([P, 1], F32)
-            nc.gpsimd.tensor_tensor(out=inv_l[:], in0=sums[:, L : L + 1], in1=minus_one[:], op=ALU.pow)
+            nc.vector.reciprocal(out=inv_l[:], in_=sums_tiles[batch][:, L : L + 1])
+            factor_tiles[batch] = inv_l
+
+        def finish_factor(batch):
+            inv_l = factor_tiles[batch]
             factor = finish_pool.tile([P, 1], F32)
-            nc.gpsimd.tensor_scalar(
-                out=factor[:], in0=sums[:, L_G : L_G + 1], scalar1=inv_l[:], scalar2=inv_l[:],
+            nc.vector.tensor_scalar(
+                out=factor[:], in0=sums_tiles[batch][:, L_G : L_G + 1], scalar1=inv_l[:], scalar2=inv_l[:],
                 op0=ALU.mult, op1=ALU.mult,
             )
-            update = finish_pool.tile([P, FEATURES], F32)
-            nc.vector.scalar_tensor_tensor(
-                out=update[:], in0=bf_bf[:, 0:FEATURES], scalar=sums[:, L_M : L_M + 1],
-                in1=sum_tiles[batch][:, 0:FEATURES], op0=ALU.mult, op1=ALU.add,
-            )
-            update_tiles[batch] = (update, factor)
+            factor_tiles[batch] = factor
 
-        def finish_statistics(batch):
-            update, factor = update_tiles[batch]
+        def finish_bias(batch):
+            biased = finish_pool.tile([P, FEATURES], F32)
+            nc.vector.scalar_tensor_tensor(
+                out=biased[:], in0=bf_bf[:, 0:FEATURES], scalar=sums_tiles[batch][:, L_M : L_M + 1],
+                in1=sum_tiles[batch, 0][:, 0:FEATURES], op0=ALU.mult, op1=ALU.add,
+            )
+            e_tiles[batch] = biased
+
+        def finish_update(batch):
+            update = finish_pool.tile([P, FEATURES], F32)
+            nc.vector.tensor_tensor(
+                out=update[:], in0=e_tiles[batch][:], in1=sum_tiles[batch, 1][:, 0:FEATURES], op=ALU.add
+            )
+            e_tiles[batch] = update
+
+        def finish_e(batch):
             e = finish_pool.tile([P, FEATURES], F32)
             nc.vector.scalar_tensor_tensor(
-                out=e[:], in0=update[:], scalar=factor[:], in1=embeds_bf[:, batch, :],
+                out=e[:], in0=e_tiles[batch][:], scalar=factor_tiles[batch][:], in1=embeds_bf[:, batch, :],
                 op0=ALU.mult, op1=ALU.add,
             )
-            stats = finish_pool.tile([P, 6], F32)
-            nc.vector.bn_stats(out=stats[:], in_=e[:])
-            mean_var = finish_pool.tile([P, 2], F32)
-            nc.vector.bn_aggr(out=mean_var[:], in_=stats[:])
-            var_eps = finish_pool.tile([P, 1], F32)
-            nc.gpsimd.tensor_scalar(
-                out=var_eps[:], in0=mean_var[:, 1:2], scalar1=LN_EPS, scalar2=1.0, op0=ALU.add, op1=ALU.mult
-            )
-            inv_std = finish_pool.tile([P, 1], F32)
-            nc.gpsimd.tensor_tensor(out=inv_std[:], in0=var_eps[:], in1=minus_half[:], op=ALU.pow)
             e_tiles[batch] = e
-            norm_tiles[batch] = (mean_var, inv_std)
 
-        def finish_norm(batch):
-            mean_var, inv_std = norm_tiles[batch]
+        def finish_stats(batch):
+            stats = finish_pool.tile([P, 6], F32)
+            nc.vector.bn_stats(out=stats[:], in_=e_tiles[batch][:])
+            norm_tiles[batch] = stats
+
+        def finish_aggregate(batches):
+            n = len(batches)
+            mean_var = finish_pool.tile([P, n, 2], F32)
+            for k, batch in enumerate(batches):
+                nc.vector.bn_aggr(out=mean_var[:, k, :], in_=norm_tiles[batch][:])
+            var_eps = finish_pool.tile([P, n], F32)
+            nc.gpsimd.tensor_scalar(
+                out=var_eps[:], in0=mean_var[:, :, 1], scalar1=LN_EPS, scalar2=1.0, op0=ALU.add, op1=ALU.mult
+            )
+            inv_std = finish_pool.tile([P, n], F32)
+            nc.gpsimd.tensor_tensor(out=inv_std[:], in0=var_eps[:], in1=minus_half[:, 0:n], op=ALU.pow)
+            for k, batch in enumerate(batches):
+                norm_tiles[batch] = (mean_var[:, k, 0:1], inv_std[:, k : k + 1])
+
+        def finish_centre(batch):
             centred = finish_pool.tile([P, FEATURES], F32)
             nc.vector.scalar_tensor_tensor(
-                out=centred[:], in0=e_tiles[batch][:], scalar=mean_var[:, 0:1], in1=gamma_bf[:],
+                out=centred[:], in0=e_tiles[batch][:], scalar=norm_tiles[batch][0], in1=gamma_bf[:],
                 op0=ALU.subtract, op1=ALU.mult,
             )
+            e_tiles[batch] = centred
+
+        def finish_store(batch):
             result = finish_pool.tile([P, FEATURES], F32)
             nc.vector.scalar_tensor_tensor(
-                out=result[:], in0=centred[:], scalar=inv_std[:], in1=beta_bf[:],
+                out=result[:], in0=e_tiles[batch][:], scalar=norm_tiles[batch][1], in1=beta_bf[:],
                 op0=ALU.mult, op1=ALU.add,
             )
             nc.sync.dma_start(out=out[batch], in_=result[:])
 
-        def in_range(s):
-            return 0 <= s < GROUPS
+        WHOLE = GROUPS - SPLIT_GROUPS
+        A, B, C, D = WHOLE, WHOLE + 1, WHOLE + 2, WHOLE + 3
 
-        def ends_batch(s):
-            return in_range(s) and s % GROUPS_PER_BATCH == GROUPS_PER_BATCH - 1
+        def batch_of(u):
+            return columns(u).start // LINKS
 
-        for i in range(-1, GROUPS + 5):
-            if in_range(i + 1):
-                transpose_x(i + 1)
-                group_x(i + 1)
-            if i >= 0 and in_range(i + X_BUFS):
-                load_x(i + X_BUFS, 1)
-            if in_range(i - 2):
-                second_matmul(i - 2)
+        def ends_batch(u):
+            return u >= 0 and columns(u).stop % LINKS == 0 and batch_of(u) < BATCHES - 2
+
+        transpose_x(0)
+        group_x(0)
+        for bank in range(len(BANKS)):
+            quantise_x(0, bank)
+        reorder_w1()
+
+        for i in range(WHOLE + 1):
+            if i >= 2:
                 gate(i - 2)
-            if in_range(i - 3):
-                link_gate(i - 3)
-                if ends_batch(i - 3):
-                    batch_terms((i - 3) // GROUPS_PER_BATCH)
-            if in_range(i - 1):
+            transpose_x(i + 1)
+            group_x(i + 1)
+            if i + X_BUFS < GROUPS:
+                load_x(i + X_BUFS, 1)
+            if i >= 1:
                 interleave_h(i - 1)
-            if in_range(i - 3):
-                link_weight(i - 3)
-            if in_range(i + 1):
-                quantise_x(i + 1, 0)
-            if in_range(i - 3):
-                add_link(i - 3, 0)
-            if in_range(i - 1):
-                quantise_h(i - 1)
-            if in_range(i - 3):
-                add_link(i - 3, 1)
-            if in_range(i + 1):
-                quantise_x(i + 1, 1)
-            if in_range(i - 3):
-                add_link(i - 3, 2)
-            if in_range(i + 1):
-                quantise_x(i + 1, 2)
-            if in_range(i - 3):
-                add_link(i - 3, 3)
-            if in_range(i + 1):
-                quantise_x(i + 1, 3)
-            if i == -1:
-                reorder_w1()
+            if i >= 2:
+                link_gate(columns(i - 2))
             if ends_batch(i - 3):
-                finish_update((i - 3) // GROUPS_PER_BATCH)
-            if ends_batch(i - 4):
-                finish_statistics((i - 4) // GROUPS_PER_BATCH)
-            if ends_batch(i - 5):
-                finish_norm((i - 5) // GROUPS_PER_BATCH)
-            if in_range(i):
+                finish_e(batch_of(i - 3))
+            quantise_x(i + 1, 0)
+            if i >= 2:
+                link_weight(columns(i - 2))
+            if i >= 1:
+                quantise_h(i - 1)
+            if ends_batch(i - 3):
+                finish_stats(batch_of(i - 3))
+            if ends_batch(i - 2):
+                finish_sums(batch_of(i - 2))
+            if i >= 2:
+                add_link(i - 2, 0)
+            quantise_x(i + 1, 1)
+            if i >= 2:
+                add_link(i - 2, 1)
+            if ends_batch(i - 3):
+                finish_aggregate([batch_of(i - 3)])
+            if ends_batch(i - 2):
+                finish_invert(batch_of(i - 2))
+            quantise_x(i + 1, 2)
+            if i >= 2:
+                add_link(i - 2, 2)
+            if ends_batch(i - 3):
+                finish_centre(batch_of(i - 3))
+            if ends_batch(i - 2):
+                finish_sum_weights(batch_of(i - 2))
+            quantise_x(i + 1, 3)
+            if i >= 2:
+                add_link(i - 2, 3)
+            if ends_batch(i - 2):
+                finish_factor(batch_of(i - 2))
+                finish_bias(batch_of(i - 2))
+            if ends_batch(i - 3):
+                finish_store(batch_of(i - 3))
+            if ends_batch(i - 2):
+                finish_update(batch_of(i - 2))
+            if i < WHOLE:
                 first_matmul(i)
+            else:
+                first_matmul(A)
+                first_matmul(B)
+            if i >= 1:
+                second_matmul(i - 1)
+
+        last = BATCHES - 1
+        gate(WHOLE - 1)
+        interleave_h(A)
+        quantise_h(A)
+        first_matmul(C)
+        second_matmul(A)
+        gate(A)
+        interleave_h(B)
+        link_gate(columns(WHOLE - 1))
+        quantise_h(B)
+        link_weight(columns(WHOLE - 1))
+        first_matmul(D)
+        second_matmul(B, from_ring=True)
+        gate(B)
+        interleave_h(C)
+        add_link(WHOLE - 1, 0)
+        add_link(WHOLE - 1, 1)
+        quantise_h(C)
+        second_matmul(C, from_ring=True)
+        gate(C)
+        add_link(WHOLE - 1, 2)
+        interleave_h(D)
+        add_link(WHOLE - 1, 3)
+        link_gate(slice(columns(A).start, columns(B).stop))
+        quantise_h(D)
+        second_matmul(D, from_ring=True)
+        gate(D)
+        link_weight(slice(columns(A).start, columns(B).stop))
+        link_gate(columns(C))
+        add_link(A, 0)
+        add_link(A, 1)
+        link_weight(columns(C))
+        add_link(B, 0)
+        add_link(B, 1)
+        link_gate(columns(D))
+        add_link(C, 0)
+        add_link(C, 1)
+        link_weight(columns(D))
+        finish_sums(last)
+        finish_sums(last - 1)
+        add_link(D, 0)
+        add_link(D, 1)
+        for step in (
+            finish_invert, finish_sum_weights, finish_factor, finish_bias, finish_update, finish_e, finish_stats
+        ):
+            step(last)
+            step(last - 1)
+        finish_aggregate([last, last - 1])
+        for step in (finish_centre, finish_store):
+            step(last)
+            step(last - 1)

@@ -198,7 +198,10 @@ def tile_embed_update_pa_t_kernel(
 
         def interleave_h(u):
             h_grouped = stage.tile([P, UNITS[u][2] * P, PACK], BF16, align_bytes=64)
-            nc.vector.tensor_copy(out=h_grouped[:], in_=hf_tiles[u][:].rearrange("p t n -> p n t"))
+            nc.vector.tensor_copy(
+                out=h_grouped[:].rearrange("p (c i) t -> p c t i", i=4),
+                in_=hf_tiles[u][:].rearrange("p t (c i) -> p c t i", i=4),
+            )
             hg_tiles[u] = h_grouped
 
         def quantise_h(u):

@@ -129,7 +129,8 @@ def tile_embed_update_pa_t_kernel(
         m_link = m_bf[:].rearrange("s b k -> s (b k)")
         sigmoid = const.tile([P, BATCHES * LINKS], F32)
         g_link = const.tile([P, BATCHES * LINKS], F32)
-        weight_link = const.tile([P, BATCHES * LINKS], F32)
+        L, L_M, L_G = 0, 1, 2
+        terms = const.tile([P, 3, BATCHES * LINKS], F32)
 
         xt_tiles, xg_tiles, xq_tiles = {}, {}, {}
         BANKS = [(pair, g) for pair in range(PAIRS) for g in range(IN_PASSES)]
@@ -247,68 +248,74 @@ def tile_embed_update_pa_t_kernel(
 
         def link_weight(cols):
             nc.vector.scalar_tensor_tensor(
-                out=weight_link[:, cols], in0=g_link[:, cols], scalar=LINK_EPS, in1=m_link[:, cols],
+                out=terms[:, L_M, cols], in0=g_link[:, cols], scalar=LINK_EPS, in1=m_link[:, cols],
                 op0=ALU.add, op1=ALU.mult,
             )
 
         def add_link(u, j):
             column = columns(u).start + j
             batch, link = divmod(column, LINKS)
-            weight = weight_link[:, column : column + 1]
-            if link < 2:
+            weight = terms[:, L_M, column : column + 1]
+            sums_of_batch = 2 if batch == BATCHES - 1 else 1
+            if link < sums_of_batch:
                 link_sum = finish_pool.tile([P, CHANNELS], F32, tag="link_sum%d" % link)
                 nc.vector.tensor_scalar(
                     out=link_sum[:], in0=o_tiles[u][:, j, :], scalar1=weight, scalar2=None, op0=ALU.mult
                 )
                 sum_tiles[batch, link] = link_sum
             else:
-                link_sum = sum_tiles[batch, link % 2]
+                link_sum = sum_tiles[batch, link % sums_of_batch]
                 nc.vector.scalar_tensor_tensor(
                     out=link_sum[:], in0=o_tiles[u][:, j, :], scalar=weight, in1=link_sum[:],
                     op0=ALU.mult, op1=ALU.add,
                 )
 
-        L, L_M, L_G = 0, 1, 2
         sums_tiles, factor_tiles, e_tiles, norm_tiles = {}, {}, {}, {}
 
-        def finish_sums(batch):
-            cols = slice(batch * LINKS, (batch + 1) * LINKS)
-            sums = finish_pool.tile([P, 3], F32)
-            terms = finish_pool.tile([P, 2, LINKS], F32)
+        def batch_columns(batches):
+            return slice(batches[0] * LINKS, (batches[-1] + 1) * LINKS)
+
+        def finish_l(batches):
+            cols = batch_columns(batches)
             nc.vector.tensor_scalar(
-                out=terms[:, 0, :], in0=g_link[:, cols], scalar1=LINK_EPS, scalar2=None,
-                op0=ALU.add, op1=ALU.add, accum_out=sums[:, L : L + 1],
+                out=terms[:, L, cols], in0=g_link[:, cols], scalar1=LINK_EPS, scalar2=None, op0=ALU.add
             )
-            nc.vector.scalar_tensor_tensor(
-                out=terms[:, 1, :], in0=g_link[:, cols], scalar=LINK_EPS, in1=g_link[:, cols],
-                op0=ALU.add, op1=ALU.mult, accum_out=sums[:, L_G : L_G + 1],
-            )
-            sums_tiles[batch] = sums
 
-        def finish_sum_weights(batch):
+        def finish_lg(batches):
+            cols = batch_columns(batches)
+            nc.vector.tensor_tensor(
+                out=terms[:, L_G, cols], in0=terms[:, L, cols], in1=g_link[:, cols], op=ALU.mult
+            )
+
+        def finish_sums(batches):
+            sums = finish_pool.tile([P, 3, len(batches)], F32)
             nc.vector.tensor_reduce(
-                out=sums_tiles[batch][:, L_M : L_M + 1],
-                in_=weight_link[:, batch * LINKS : (batch + 1) * LINKS], axis=AXIS.X, op=ALU.add,
+                out=sums[:], in_=terms[:, :, batch_columns(batches)].rearrange("p k (b l) -> p k b l", l=LINKS),
+                axis=AXIS.X, op=ALU.add,
             )
+            for k, batch in enumerate(batches):
+                sums_tiles[batch] = (sums, k)
 
-        def finish_invert(batch):
-            inv_l = finish_pool.tile([P, 1], F32)
-            nc.vector.reciprocal(out=inv_l[:], in_=sums_tiles[batch][:, L : L + 1])
-            factor_tiles[batch] = inv_l
+        def finish_invert(batches):
+            inv_l = finish_pool.tile([P, len(batches)], F32)
+            nc.vector.reciprocal(out=inv_l[:], in_=sums_tiles[batches[0]][0][:, L, :])
+            for k, batch in enumerate(batches):
+                factor_tiles[batch] = inv_l[:, k : k + 1]
 
         def finish_factor(batch):
+            sums, k = sums_tiles[batch]
             inv_l = factor_tiles[batch]
             factor = finish_pool.tile([P, 1], F32)
             nc.vector.tensor_scalar(
-                out=factor[:], in0=sums_tiles[batch][:, L_G : L_G + 1], scalar1=inv_l[:], scalar2=inv_l[:],
-                op0=ALU.mult, op1=ALU.mult,
+                out=factor[:], in0=sums[:, L_G, k : k + 1], scalar1=inv_l, scalar2=inv_l, op0=ALU.mult, op1=ALU.mult
             )
-            factor_tiles[batch] = factor
+            factor_tiles[batch] = factor[:]
 
         def finish_bias(batch):
             biased = finish_pool.tile([P, FEATURES], F32)
             nc.vector.scalar_tensor_tensor(
-                out=biased[:], in0=bf_bf[:, 0:FEATURES], scalar=sums_tiles[batch][:, L_M : L_M + 1],
+                out=biased[:], in0=bf_bf[:, 0:FEATURES],
+                scalar=sums_tiles[batch][0][:, L_M, sums_tiles[batch][1] : sums_tiles[batch][1] + 1],
                 in1=sum_tiles[batch, 0][:, 0:FEATURES], op0=ALU.mult, op1=ALU.add,
             )
             e_tiles[batch] = biased
@@ -323,7 +330,7 @@ def tile_embed_update_pa_t_kernel(
         def finish_e(batch):
             e = finish_pool.tile([P, FEATURES], F32)
             nc.vector.scalar_tensor_tensor(
-                out=e[:], in0=e_tiles[batch][:], scalar=factor_tiles[batch][:], in1=embeds_bf[:, batch, :],
+                out=e[:], in0=e_tiles[batch][:], scalar=factor_tiles[batch], in1=embeds_bf[:, batch, :],
                 op0=ALU.mult, op1=ALU.add,
             )
             e_tiles[batch] = e
@@ -333,11 +340,19 @@ def tile_embed_update_pa_t_kernel(
             nc.vector.bn_stats(out=stats[:], in_=e_tiles[batch][:])
             norm_tiles[batch] = stats
 
-        def finish_aggregate(batches):
+        def finish_aggregate(batches, on_scalar=False):
             n = len(batches)
             mean_var = finish_pool.tile([P, n, 2], F32)
             for k, batch in enumerate(batches):
                 nc.vector.bn_aggr(out=mean_var[:, k, :], in_=norm_tiles[batch][:])
+            if on_scalar:
+                inv_std = finish_pool.tile([P, n], F32)
+                nc.scalar.activation(
+                    out=inv_std[:], in_=mean_var[:, :, 1], func=ACT.Abs_reciprocal_sqrt, bias=LN_EPS
+                )
+                for k, batch in enumerate(batches):
+                    norm_tiles[batch] = (mean_var[:, k, 0:1], inv_std[:, k : k + 1])
+                return
             var_eps = finish_pool.tile([P, n], F32)
             nc.gpsimd.tensor_scalar(
                 out=var_eps[:], in0=mean_var[:, :, 1], scalar1=LN_EPS, scalar2=1.0, op0=ALU.add, op1=ALU.mult
@@ -385,47 +400,50 @@ def tile_embed_update_pa_t_kernel(
             group_x(i + 1)
             if i + X_BUFS < GROUPS:
                 load_x(i + X_BUFS, 1)
+            ended = [batch_of(i - 2)] if ends_batch(i - 2) else []
+            ended_before = [batch_of(i - 3)] if ends_batch(i - 3) else []
             if i >= 1:
                 interleave_h(i - 1)
             if i >= 2:
                 link_gate(columns(i - 2))
-            if ends_batch(i - 3):
-                finish_e(batch_of(i - 3))
+            for batch in ended_before:
+                finish_e(batch)
             quantise_x(i + 1, 0)
             if i >= 2:
                 link_weight(columns(i - 2))
+            if ended:
+                finish_l(ended)
             if i >= 1:
                 quantise_h(i - 1)
-            if ends_batch(i - 3):
-                finish_stats(batch_of(i - 3))
-            if ends_batch(i - 2):
-                finish_sums(batch_of(i - 2))
+            for batch in ended_before:
+                finish_stats(batch)
+            if ended:
+                finish_lg(ended)
             if i >= 2:
                 add_link(i - 2, 0)
             quantise_x(i + 1, 1)
             if i >= 2:
                 add_link(i - 2, 1)
-            if ends_batch(i - 3):
-                finish_aggregate([batch_of(i - 3)])
-            if ends_batch(i - 2):
-                finish_invert(batch_of(i - 2))
+            if ended_before:
+                finish_aggregate(ended_before)
+            if ended:
+                finish_sums(ended)
             quantise_x(i + 1, 2)
-            if i >= 2:
+            if 2 <= i < WHOLE:
                 add_link(i - 2, 2)
-            if ends_batch(i - 3):
-                finish_centre(batch_of(i - 3))
-            if ends_batch(i - 2):
-                finish_sum_weights(batch_of(i - 2))
+            for batch in ended_before:
+                finish_centre(batch)
+            if ended:
+                finish_invert(ended)
             quantise_x(i + 1, 3)
-            if i >= 2:
+            if 2 <= i < WHOLE:
                 add_link(i - 2, 3)
-            if ends_batch(i - 2):
-                finish_factor(batch_of(i - 2))
-                finish_bias(batch_of(i - 2))
-            if ends_batch(i - 3):
-                finish_store(batch_of(i - 3))
-            if ends_batch(i - 2):
-                finish_update(batch_of(i - 2))
+            for batch in ended:
+                finish_factor(batch)
+            for batch in ended_before:
+                finish_store(batch)
+            for batch in ended:
+                finish_bias(batch)
             if i < WHOLE:
                 first_matmul(i)
             else:
@@ -435,17 +453,20 @@ def tile_embed_update_pa_t_kernel(
                 second_matmul(i - 1)
 
         last = BATCHES - 1
+        both = [last - 1, last]
         gate(WHOLE - 1)
         interleave_h(A)
+        add_link(WHOLE - 2, 2)
+        add_link(WHOLE - 2, 3)
         quantise_h(A)
         first_matmul(C)
-        second_matmul(A)
-        gate(A)
         interleave_h(B)
         link_gate(columns(WHOLE - 1))
         quantise_h(B)
         link_weight(columns(WHOLE - 1))
         first_matmul(D)
+        second_matmul(A, from_ring=True)
+        gate(A)
         second_matmul(B, from_ring=True)
         gate(B)
         interleave_h(C)
@@ -457,31 +478,36 @@ def tile_embed_update_pa_t_kernel(
         add_link(WHOLE - 1, 2)
         interleave_h(D)
         add_link(WHOLE - 1, 3)
-        link_gate(slice(columns(A).start, columns(B).stop))
+        link_gate(slice(columns(A).start, columns(C).stop))
         quantise_h(D)
         second_matmul(D, from_ring=True)
         gate(D)
-        link_weight(slice(columns(A).start, columns(B).stop))
-        link_gate(columns(C))
+        nc.scalar.activation(out=table_warmer[:], in_=minus_half[:, 0:1], func=ACT.Abs_reciprocal_sqrt)
+        link_weight(slice(columns(A).start, columns(C).stop))
         add_link(A, 0)
         add_link(A, 1)
-        link_weight(columns(C))
         add_link(B, 0)
         add_link(B, 1)
         link_gate(columns(D))
         add_link(C, 0)
-        add_link(C, 1)
+        finish_l(both)
         link_weight(columns(D))
-        finish_sums(last)
-        finish_sums(last - 1)
+        add_link(C, 1)
+        finish_lg(both)
         add_link(D, 0)
         add_link(D, 1)
-        for step in (
-            finish_invert, finish_sum_weights, finish_factor, finish_bias, finish_update, finish_e, finish_stats
-        ):
-            step(last)
-            step(last - 1)
-        finish_aggregate([last, last - 1])
+        finish_sums(both)
+        finish_invert(both)
+        finish_bias(last - 1)
+        finish_bias(last)
+        finish_factor(last - 1)
+        finish_factor(last)
+        finish_update(last)
+        finish_e(last - 1)
+        finish_e(last)
+        finish_stats(last - 1)
+        finish_stats(last)
+        finish_aggregate([last, last - 1], on_scalar=True)
         for step in (finish_centre, finish_store):
             step(last)
             step(last - 1)

@@ -41,6 +41,8 @@ def tile_embed_update_pa_t_kernel(
     tc, net_in, embeds, m, W1_words, W1_scales, b1, Wf_words, Wf_scales, b_f, gamma, beta, out
 ):
     nc = tc.nc
+    net_in_rows = net_in.rearrange("b s k i -> (b s) k i").rearrange("(p b) k i -> b p k i", b=BATCHES)
+    out_rows = out.rearrange("b s c -> (b s) c").rearrange("(p b) c -> p b c", b=BATCHES)
     with ExitStack() as ctx:
         ctx.enter_context(tc.manual_schedule())
         const = ctx.enter_context(tc.tile_pool(name="const", bufs=1))
@@ -67,7 +69,7 @@ def tile_embed_update_pa_t_kernel(
             for h in range(pieces):
                 nc.sync.dma_start(
                     out=x_rows[:, h * step : (h + 1) * step, :],
-                    in_=net_in[batch, :, first_link + h * step : first_link + (h + 1) * step, :],
+                    in_=net_in_rows[batch, :, first_link + h * step : first_link + (h + 1) * step, :],
                 )
             x_tiles[s] = x_rows
 
@@ -101,7 +103,7 @@ def tile_embed_update_pa_t_kernel(
         bf_bf = const.tile([P, CHANNELS], BF16)
         nc.sync.dma_start(out=bf_bf[:], in_=b_f.partition_broadcast(P))
         m_bf = const.tile([P, BATCHES, LINKS], BF16)
-        nc.sync.dma_start(out=m_bf[:], in_=m.rearrange("b s k o -> s b (k o)"))
+        nc.sync.dma_start(out=m_bf[:], in_=m.rearrange("b s k o -> (b s) (k o)").rearrange("(p b) k -> p b k", b=BATCHES))
         load_x(3, 1)
         load_x(4, 1)
         gamma_bf = const.tile([P, FEATURES], BF16)
@@ -109,7 +111,7 @@ def tile_embed_update_pa_t_kernel(
         beta_bf = const.tile([P, FEATURES], BF16)
         nc.sync.dma_start(out=beta_bf[:], in_=beta.partition_broadcast(P))
         embeds_bf = const.tile([P, BATCHES, FEATURES], BF16)
-        nc.sync.dma_start(out=embeds_bf[:], in_=embeds.rearrange("b s c -> s b c"))
+        nc.sync.dma_start(out=embeds_bf[:], in_=embeds.rearrange("b s c -> (b s) c").rearrange("(p b) c -> p b c", b=BATCHES))
         for s in range(5, X_BUFS):
             load_x(s, 1)
 
@@ -271,6 +273,7 @@ def tile_embed_update_pa_t_kernel(
                 )
 
         sums_tiles, factor_tiles, e_tiles, norm_tiles = {}, {}, {}, {}
+        result = const.tile([P, BATCHES, FEATURES], F32)
 
         def batch_columns(batches):
             return slice(batches[0] * LINKS, (batches[-1] + 1) * LINKS)
@@ -370,13 +373,15 @@ def tile_embed_update_pa_t_kernel(
             )
             e_tiles[batch] = centred
 
-        def finish_store(batch):
-            result = finish_pool.tile([P, FEATURES], F32)
+        def finish_scale(batch):
             nc.vector.scalar_tensor_tensor(
-                out=result[:], in0=e_tiles[batch][:], scalar=norm_tiles[batch][1], in1=beta_bf[:],
+                out=result[:, batch, :], in0=e_tiles[batch][:], scalar=norm_tiles[batch][1], in1=beta_bf[:],
                 op0=ALU.mult, op1=ALU.add,
             )
-            nc.sync.dma_start(out=out[batch], in_=result[:])
+
+        def store(batches):
+            rows = slice(batches[0], batches[-1] + 1)
+            nc.sync.dma_start(out=out_rows[:, rows, :], in_=result[:, rows, :])
 
         WHOLE = GROUPS - SPLIT_GROUPS
         A, B, C, D = WHOLE, WHOLE + 1, WHOLE + 2, WHOLE + 3
@@ -441,7 +446,8 @@ def tile_embed_update_pa_t_kernel(
             for batch in ended:
                 finish_factor(batch)
             for batch in ended_before:
-                finish_store(batch)
+                finish_scale(batch)
+                store([batch])
             for batch in ended:
                 finish_bias(batch)
             if i < WHOLE:
@@ -508,6 +514,7 @@ def tile_embed_update_pa_t_kernel(
         finish_stats(last - 1)
         finish_stats(last)
         finish_aggregate([last, last - 1], on_scalar=True)
-        for step in (finish_centre, finish_store):
+        for step in (finish_centre, finish_scale):
             step(last)
             step(last - 1)
+        store(both)

@@ -20,6 +20,10 @@ PACK = 4
 K_PASS = PACK * P
 PASS_WORDS = K_PASS // 2
 IN_PASSES = IN // K_PASS
+ROW_FLOATS = BATCHES * FEATURES
+OVERHANG = 4
+EVEN_START = 248
+ODD_START = 252
 LN_EPS = 1e-5
 LINK_EPS = 1e-8
 
@@ -42,7 +46,8 @@ def tile_embed_update_pa_t_kernel(
 ):
     nc = tc.nc
     net_in_rows = net_in.rearrange("b s k i -> (b s) k i").rearrange("(p b) k i -> b p k i", b=BATCHES)
-    out_rows = out.rearrange("b s c -> (b s) c").rearrange("(p b) c -> p b c", b=BATCHES)
+    out_rows = out.rearrange("b s c -> (b s c)").rearrange("(p f) -> p f", p=P)
+    out_pairs = out.rearrange("b s c -> (b s c)").rearrange("(q f) -> q f", q=P // 2)
     with ExitStack() as ctx:
         ctx.enter_context(tc.manual_schedule())
         const = ctx.enter_context(tc.tile_pool(name="const", bufs=1))
@@ -273,7 +278,7 @@ def tile_embed_update_pa_t_kernel(
                 )
 
         sums_tiles, factor_tiles, e_tiles, norm_tiles = {}, {}, {}, {}
-        result = const.tile([P, BATCHES, FEATURES], F32)
+        result = const.tile([P, ROW_FLOATS + OVERHANG], F32)
 
         def batch_columns(batches):
             return slice(batches[0] * LINKS, (batches[-1] + 1) * LINKS)
@@ -375,13 +380,24 @@ def tile_embed_update_pa_t_kernel(
 
         def finish_scale(batch):
             nc.vector.scalar_tensor_tensor(
-                out=result[:, batch, :], in0=e_tiles[batch][:], scalar=norm_tiles[batch][1], in1=beta_bf[:],
+                out=result[:, batch * FEATURES : (batch + 1) * FEATURES], in0=e_tiles[batch][:], scalar=norm_tiles[batch][1], in1=beta_bf[:],
                 op0=ALU.mult, op1=ALU.add,
             )
 
-        def store(batches):
-            rows = slice(batches[0], batches[-1] + 1)
-            nc.sync.dma_start(out=out_rows[:, rows, :], in_=result[:, rows, :])
+        def store(batch):
+            cols = slice(batch * FEATURES, (batch + 1) * FEATURES)
+            nc.sync.dma_start(out=out_rows[:, cols], in_=result[:, cols])
+
+        def fetch_overhang():
+            nc.sync.dma_start(
+                out=result[0::2, ROW_FLOATS:], in_=out_pairs[:, ROW_FLOATS : ROW_FLOATS + OVERHANG]
+            )
+
+        def store_last_two():
+            nc.sync.dma_start(out=out_pairs[:, EVEN_START : ROW_FLOATS + OVERHANG], in_=result[0::2, EVEN_START:])
+            nc.scalar.dma_start(
+                out=out_pairs[:, ROW_FLOATS + ODD_START :], in_=result[1::2, ODD_START:ROW_FLOATS]
+            )
 
         WHOLE = GROUPS - SPLIT_GROUPS
         A, B, C, D = WHOLE, WHOLE + 1, WHOLE + 2, WHOLE + 3
@@ -447,9 +463,11 @@ def tile_embed_update_pa_t_kernel(
                 finish_factor(batch)
             for batch in ended_before:
                 finish_scale(batch)
-                store([batch])
+                store(batch)
             for batch in ended:
                 finish_bias(batch)
+            if i == GROUPS // 2:
+                fetch_overhang()
             if i < WHOLE:
                 first_matmul(i)
             else:
@@ -517,4 +535,4 @@ def tile_embed_update_pa_t_kernel(
         for step in (finish_centre, finish_scale):
             step(last)
             step(last - 1)
-        store(both)
+        store_last_two()

@@ -92,19 +92,19 @@ def tile_embed_update_pa_t_kernel(
 
         load_x(0, PAIRS)
         load_scales(w1_scales_raw, W1_scales.rearrange("g r n -> r g n"))
+        load_x(1, PAIRS)
         w1_raw = const.tile([P, IN_PASSES, HID], I32, align_bytes=64)
         nc.sync.dma_start(
             out=w1_raw[:], in_=W1_words.rearrange("g p n t -> p g (n t)").bitcast(I32)
         )
         b1_bf = const.tile([P, PACK], BF16)
         nc.sync.dma_start(out=b1_bf[:], in_=b1.rearrange("(p t) -> p t", t=PACK))
-        load_x(1, PAIRS)
+        load_x(2, 1)
         wf_words = const.tile([P, 4 * CHANNELS], U8, align_bytes=64)
         nc.sync.dma_start(
             out=wf_words[:].bitcast(I32), in_=Wf_words[0].rearrange("p n t -> p (n t)").bitcast(I32)
         )
         load_scales(wf_scales, Wf_scales[0])
-        load_x(2, 1)
         bf_bf = const.tile([P, CHANNELS], BF16)
         nc.sync.dma_start(out=bf_bf[:], in_=b_f.partition_broadcast(P))
         m_bf = const.tile([P, BATCHES, LINKS], BF16)
@@ -123,14 +123,16 @@ def tile_embed_update_pa_t_kernel(
         w1_words = const.tile([P, IN_PASSES, PACK, P], I32, align_bytes=64)
         w1_scales = const.tile([P, IN_PASSES, PACK, P], U8, align_bytes=64)
 
-        def reorder_w1():
+        def reorder_w1_scales():
             for g in range(IN_PASSES):
                 nc.vector.tensor_copy(
                     out=w1_scales[:, g], in_=w1_scales_raw[:, g, :].rearrange("p (c t) -> p t c", t=PACK)
                 )
-            for g in range(IN_PASSES):
+
+        def reorder_w1_words():
+            for t in range(PACK):
                 nc.vector.tensor_copy(
-                    out=w1_words[:, g], in_=w1_raw[:, g, :].rearrange("p (c t) -> p t c", t=PACK)
+                    out=w1_words[:, :, t, :], in_=w1_raw[:].rearrange("p g (c t) -> p g c t", t=PACK)[:, :, :, t]
                 )
 
         m_link = m_bf[:].rearrange("s b k -> s (b k)")
@@ -412,7 +414,9 @@ def tile_embed_update_pa_t_kernel(
         group_x(0)
         for bank in range(len(BANKS)):
             quantise_x(0, bank)
-        reorder_w1()
+        reorder_w1_scales()
+
+        reorder_w1_words()
 
         for i in range(WHOLE + 1):
             if i >= 2:

@@ -142,10 +142,14 @@ def tile_embed_update_pa_t_kernel(
         terms = const.tile([P, 3, BATCHES * LINKS], F32)
 
         xt_tiles, xg_tiles, xq_tiles = {}, {}, {}
-        BANKS = [(pair, g) for pair in range(PAIRS) for g in range(IN_PASSES)]
+
+        def banks(s):
+            if s < 2:
+                return [(pair, g) for pair in range(PAIRS) for g in range(IN_PASSES)]
+            return [(pair, g) for g in range(IN_PASSES) for pair in range(PAIRS)]
 
         def transpose_x(s):
-            for pair, g in BANKS:
+            for pair, g in banks(s):
                 x_t = psum.tile([P, 2, 2, P], F32, tag="bank")
                 for j in range(2):
                     words = x_tiles[s][:, 2 * pair + j, :].bitcast(F32)
@@ -159,7 +163,7 @@ def tile_embed_update_pa_t_kernel(
 
         def group_x(s):
             x_grouped = stage.tile([P, IN_PASSES, GROUP_TILES, P, PACK], BF16, align_bytes=64)
-            for pair, g in BANKS:
+            for pair, g in banks(s):
                 nc.scalar.copy(
                     out=x_grouped[:, g, 2 * pair : 2 * pair + 2].bitcast(F32),
                     in_=xt_tiles[s, pair, g][:].rearrange("p j u t -> p j t u"),
@@ -169,10 +173,8 @@ def tile_embed_update_pa_t_kernel(
             x_scales = stage.tile([P, IN_PASSES, GROUP_TILES, P], U8, align_bytes=64)
             xq_tiles[s] = (x_codes, x_scales)
 
-        def quantise_x(s, bank):
-            pair, g = BANKS[bank]
+        def quantise_x(s, g, tiles=slice(0, GROUP_TILES)):
             x_codes, x_scales = xq_tiles[s]
-            tiles = slice(2 * pair, 2 * pair + 2)
             nc.vector.quantize_mx(
                 out=x_codes[:, g, tiles].rearrange("p j t -> p (j t)").bitcast(FP8X4),
                 scales=x_scales[:, g, tiles].rearrange("p j t -> p (j t)"),
@@ -265,7 +267,7 @@ def tile_embed_update_pa_t_kernel(
             column = columns(u).start + j
             batch, link = divmod(column, LINKS)
             weight = terms[:, L_M, column : column + 1]
-            sums_of_batch = 2 if batch == BATCHES - 1 else 1
+            sums_of_batch = 2
             if link < sums_of_batch:
                 link_sum = finish_pool.tile([P, CHANNELS], F32, tag="link_sum%d" % link)
                 nc.vector.tensor_scalar(
@@ -323,17 +325,18 @@ def tile_embed_update_pa_t_kernel(
 
         def finish_bias(batch):
             biased = finish_pool.tile([P, FEATURES], F32)
+            link_sum = e_tiles[batch]
             nc.vector.scalar_tensor_tensor(
                 out=biased[:], in0=bf_bf[:, 0:FEATURES],
                 scalar=sums_tiles[batch][0][:, L_M, sums_tiles[batch][1] : sums_tiles[batch][1] + 1],
-                in1=sum_tiles[batch, 0][:, 0:FEATURES], op0=ALU.mult, op1=ALU.add,
+                in1=link_sum[:, 0:FEATURES], op0=ALU.mult, op1=ALU.add,
             )
             e_tiles[batch] = biased
 
         def finish_update(batch):
             update = finish_pool.tile([P, FEATURES], F32)
             nc.vector.tensor_tensor(
-                out=update[:], in0=e_tiles[batch][:], in1=sum_tiles[batch, 1][:, 0:FEATURES], op=ALU.add
+                out=update[:], in0=sum_tiles[batch, 0][:, 0:FEATURES], in1=sum_tiles[batch, 1][:, 0:FEATURES], op=ALU.add
             )
             e_tiles[batch] = update
 
@@ -412,8 +415,8 @@ def tile_embed_update_pa_t_kernel(
 
         transpose_x(0)
         group_x(0)
-        for bank in range(len(BANKS)):
-            quantise_x(0, bank)
+        for pair, g in banks(0):
+            quantise_x(0, g, slice(2 * pair, 2 * pair + 2))
         reorder_w1_scales()
 
         reorder_w1_words()
@@ -432,10 +435,16 @@ def tile_embed_update_pa_t_kernel(
             if i >= 2:
                 link_gate(columns(i - 2))
             for batch in ended_before:
-                finish_e(batch)
-            quantise_x(i + 1, 0)
+                finish_bias(batch)
+            if i == 0:
+                for pair, g in banks(1):
+                    quantise_x(1, g, slice(2 * pair, 2 * pair + 2))
+            else:
+                quantise_x(i + 1, 0)
             if i >= 2:
                 link_weight(columns(i - 2))
+            for batch in ended_before:
+                finish_e(batch)
             if ended:
                 finish_l(ended)
             if i >= 1:
@@ -446,30 +455,26 @@ def tile_embed_update_pa_t_kernel(
                 finish_lg(ended)
             if i >= 2:
                 add_link(i - 2, 0)
-            quantise_x(i + 1, 1)
-            if i >= 2:
                 add_link(i - 2, 1)
             if ended_before:
                 finish_aggregate(ended_before)
             if ended:
                 finish_sums(ended)
-            quantise_x(i + 1, 2)
-            if 2 <= i < WHOLE:
-                add_link(i - 2, 2)
+            if i >= 1:
+                quantise_x(i + 1, 1)
             for batch in ended_before:
                 finish_centre(batch)
             if ended:
                 finish_invert(ended)
-            quantise_x(i + 1, 3)
             if 2 <= i < WHOLE:
+                add_link(i - 2, 2)
                 add_link(i - 2, 3)
-            for batch in ended:
-                finish_factor(batch)
             for batch in ended_before:
                 finish_scale(batch)
                 store(batch)
             for batch in ended:
-                finish_bias(batch)
+                finish_factor(batch)
+                finish_update(batch)
             if i == GROUPS // 2:
                 fetch_overhang()
             if i < WHOLE:
@@ -526,11 +531,12 @@ def tile_embed_update_pa_t_kernel(
         add_link(D, 1)
         finish_sums(both)
         finish_invert(both)
+        finish_update(last - 1)
+        finish_update(last)
+        finish_factor(last - 1)
         finish_bias(last - 1)
         finish_bias(last)
-        finish_factor(last - 1)
         finish_factor(last)
-        finish_update(last)
         finish_e(last - 1)
         finish_e(last)
         finish_stats(last - 1)

@@ -266,8 +266,8 @@ def tile_embed_update_pa_t_kernel(
         def add_link(u, j):
             column = columns(u).start + j
             batch, link = divmod(column, LINKS)
-            weight = terms[:, L_M, column : column + 1]
-            sums_of_batch = 2
+            weight = last_lm[:, link : link + 1] if u == D else terms[:, L_M, column : column + 1]
+            sums_of_batch = 1 if u >= WHOLE - 1 else 2
             if link < sums_of_batch:
                 link_sum = finish_pool.tile([P, CHANNELS], F32, tag="link_sum%d" % link)
                 nc.vector.tensor_scalar(
@@ -280,6 +280,24 @@ def tile_embed_update_pa_t_kernel(
                     out=link_sum[:], in0=o_tiles[u][:, j, :], scalar=weight, in1=link_sum[:],
                     op0=ALU.mult, op1=ALU.add,
                 )
+
+        scaled_tiles = []
+
+        def scale_link(u, j):
+            scaled = finish_pool.tile([P, CHANNELS], F32, bufs=6)
+            column = columns(u).start + j
+            nc.scalar.activation(
+                out=scaled[:], in_=o_tiles[u][:, j, :], func=ACT.Copy, scale=terms[:, L_M, column : column + 1]
+            )
+            scaled_tiles.append(scaled)
+
+        def sum_scaled(first, last):
+            for n, scaled in enumerate(scaled_tiles):
+                nc.tensor.matmul(
+                    out=tensor_sum[:], lhsT=identity[:], rhs=scaled[:],
+                    start=first and n == 0, stop=last and n == len(scaled_tiles) - 1,
+                )
+            scaled_tiles.clear()
 
         sums_tiles, factor_tiles, e_tiles, norm_tiles = {}, {}, {}, {}
         result = const.tile([P, ROW_FLOATS + OVERHANG], F32)
@@ -313,6 +331,76 @@ def tile_embed_update_pa_t_kernel(
             nc.vector.reciprocal(out=inv_l[:], in_=sums_tiles[batches[0]][0][:, L, :])
             for k, batch in enumerate(batches):
                 factor_tiles[batch] = inv_l[:, k : k + 1]
+
+        def last_gates(batch):
+            cols = batch_columns([batch])
+            nc.vector.scalar_tensor_tensor(
+                out=last_g[:], in0=sigmoid[:, cols], scalar=1.0, in1=m_link[:, cols],
+                op0=ALU.mult, op1=ALU.mult, accum_out=last_sums[:, 0:1],
+            )
+
+        def last_weights(batch):
+            cols = batch_columns([batch])
+            nc.vector.scalar_tensor_tensor(
+                out=last_lm[:], in0=last_g[:], scalar=LINK_EPS, in1=m_link[:, cols],
+                op0=ALU.add, op1=ALU.mult, accum_out=last_sums[:, 1:2],
+            )
+
+        def last_l(batch):
+            nc.vector.tensor_scalar(
+                out=last_sums[:, 3:4], in0=last_sums[:, 0:1], scalar1=LINKS * LINK_EPS, scalar2=None, op0=ALU.add
+            )
+
+        def last_squares(batch):
+            cols = batch_columns([batch])
+            nc.vector.scalar_tensor_tensor(
+                out=last_lg[:], in0=last_g[:], scalar=LINK_EPS, in1=last_g[:],
+                op0=ALU.add, op1=ALU.mult, accum_out=last_sums[:, 2:3],
+            )
+
+        def last_invert(batch):
+            nc.vector.reciprocal(out=last_sums[:, 4:5], in_=last_sums[:, 3:4])
+
+        def last_factor(batch):
+            nc.vector.tensor_scalar(
+                out=last_sums[:, 5:6], in0=last_sums[:, 2:3], scalar1=last_sums[:, 4:5], scalar2=last_sums[:, 4:5],
+                op0=ALU.mult, op1=ALU.mult,
+            )
+            factor_tiles[batch] = last_sums[:, 5:6]
+
+        def last_bias(batch):
+            biased = finish_pool.tile([P, FEATURES], F32)
+            nc.vector.scalar_tensor_tensor(
+                out=biased[:], in0=bf_bf[:, 0:FEATURES], scalar=last_sums[:, 1:2],
+                in1=sum_tiles[batch, 0][:, 0:FEATURES], op0=ALU.mult, op1=ALU.add,
+            )
+            e_tiles[batch] = biased
+
+        def last_tensor_part(batch):
+            part = finish_pool.tile([P, FEATURES], F32)
+            nc.vector.scalar_tensor_tensor(
+                out=part[:], in0=tensor_sum[:, 0:FEATURES], scalar=factor_tiles[batch], in1=embeds_bf[:, batch, :],
+                op0=ALU.mult, op1=ALU.add,
+            )
+            sum_tiles[batch, 2] = part
+
+        def last_e(batch):
+            e = finish_pool.tile([P, FEATURES], F32)
+            nc.vector.scalar_tensor_tensor(
+                out=e[:], in0=e_tiles[batch][:], scalar=factor_tiles[batch], in1=sum_tiles[batch, 2][:],
+                op0=ALU.mult, op1=ALU.add,
+            )
+            e_tiles[batch] = e
+
+        def last_merge(batch):
+            nc.vector.tensor_tensor(
+                out=sum_tiles[batch, 0][:], in0=sum_tiles[batch, 0][:], in1=sum_tiles[batch, 1][:], op=ALU.add
+            )
+
+        last_sums = const.tile([P, 6], F32)
+        last_g = const.tile([P, LINKS], F32)
+        last_lm = const.tile([P, LINKS], F32)
+        last_lg = const.tile([P, LINKS], F32)
 
         def finish_factor(batch):
             sums, k = sums_tiles[batch]
@@ -411,7 +499,7 @@ def tile_embed_update_pa_t_kernel(
             return columns(u).start // LINKS
 
         def ends_batch(u):
-            return u >= 0 and columns(u).stop % LINKS == 0 and batch_of(u) < BATCHES - 2
+            return u >= 0 and columns(u).stop % LINKS == 0 and batch_of(u) < BATCHES - 1
 
         transpose_x(0)
         group_x(0)
@@ -429,7 +517,7 @@ def tile_embed_update_pa_t_kernel(
             if i + X_BUFS < GROUPS:
                 load_x(i + X_BUFS, 1)
             ended = [batch_of(i - 2)] if ends_batch(i - 2) else []
-            ended_before = [batch_of(i - 3)] if ends_batch(i - 3) else []
+            ended_before = [batch_of(i - 3)] if ends_batch(i - 3) and i < WHOLE else []
             if i >= 1:
                 interleave_h(i - 1)
             if i >= 2:
@@ -486,63 +574,64 @@ def tile_embed_update_pa_t_kernel(
                 second_matmul(i - 1)
 
         last = BATCHES - 1
-        both = [last - 1, last]
-        gate(WHOLE - 1)
+        U = WHOLE - 1
+        gate(U)
         interleave_h(A)
-        add_link(WHOLE - 2, 2)
-        add_link(WHOLE - 2, 3)
+        add_link(U - 1, 2)
+        add_link(U - 1, 3)
         quantise_h(A)
         first_matmul(C)
         interleave_h(B)
-        link_gate(columns(WHOLE - 1))
+        link_gate(columns(U))
         quantise_h(B)
-        link_weight(columns(WHOLE - 1))
+        link_weight(columns(U))
         first_matmul(D)
         second_matmul(A, from_ring=True)
         gate(A)
         second_matmul(B, from_ring=True)
         gate(B)
         interleave_h(C)
-        add_link(WHOLE - 1, 0)
-        add_link(WHOLE - 1, 1)
+        finish_bias(last - 1)
+        last_merge(last)
         quantise_h(C)
         second_matmul(C, from_ring=True)
+        for j in range(GROUP_TILES):
+            scale_link(U, j)
         gate(C)
-        add_link(WHOLE - 1, 2)
+        tensor_sum = psum.tile([P, CHANNELS], F32, tag="bank")
+        sum_scaled(True, False)
         interleave_h(D)
-        add_link(WHOLE - 1, 3)
-        link_gate(slice(columns(A).start, columns(C).stop))
+        link_gate(slice(columns(A).start, columns(B).stop))
         quantise_h(D)
         second_matmul(D, from_ring=True)
+        link_weight(slice(columns(A).start, columns(B).stop))
+        link_gate(columns(C))
+        scale_link(A, 0)
+        scale_link(A, 1)
         gate(D)
-        nc.scalar.activation(out=table_warmer[:], in_=minus_half[:, 0:1], func=ACT.Abs_reciprocal_sqrt)
-        link_weight(slice(columns(A).start, columns(C).stop))
-        add_link(A, 0)
-        add_link(A, 1)
-        add_link(B, 0)
-        add_link(B, 1)
-        link_gate(columns(D))
-        add_link(C, 0)
-        finish_l(both)
-        link_weight(columns(D))
-        add_link(C, 1)
-        finish_lg(both)
-        add_link(D, 0)
-        add_link(D, 1)
-        finish_sums(both)
-        finish_invert(both)
-        finish_update(last - 1)
-        finish_update(last)
-        finish_factor(last - 1)
-        finish_bias(last - 1)
-        finish_bias(last)
-        finish_factor(last)
         finish_e(last - 1)
-        finish_e(last)
+        link_weight(columns(C))
+        for u, j in ((B, 0), (B, 1), (C, 0), (C, 1)):
+            scale_link(u, j)
+        nc.scalar.activation(out=table_warmer[:], in_=minus_half[:, 0:1], func=ACT.Abs_reciprocal_sqrt)
+        sum_scaled(False, True)
+        last_gates(last)
         finish_stats(last - 1)
+        last_weights(last)
+        last_l(last)
+        last_squares(last)
+        add_link(D, 0)
+        last_invert(last)
+        add_link(D, 1)
+        last_factor(last)
+        finish_aggregate([last - 1], on_scalar=True)
+        last_tensor_part(last)
+        last_bias(last)
+        finish_centre(last - 1)
+        last_e(last)
+        finish_scale(last - 1)
         finish_stats(last)
-        finish_aggregate([last, last - 1], on_scalar=True)
-        for step in (finish_centre, finish_scale):
-            step(last)
-            step(last - 1)
+        finish_aggregate([last], on_scalar=True)
+        finish_centre(last)
+        finish_scale(last)
         store_last_two()

@@ -518,6 +518,7 @@ def tile_embed_update_pa_t_kernel(
                 load_x(i + X_BUFS, 1)
             ended = [batch_of(i - 2)] if ends_batch(i - 2) else []
             ended_before = [batch_of(i - 3)] if ends_batch(i - 3) and i < WHOLE else []
+            ended_long = [batch_of(i - 4)] if ends_batch(i - 4) else []
             if i >= 1:
                 interleave_h(i - 1)
             if i >= 2:
@@ -557,7 +558,7 @@ def tile_embed_update_pa_t_kernel(
             if 2 <= i < WHOLE:
                 add_link(i - 2, 2)
                 add_link(i - 2, 3)
-            for batch in ended_before:
+            for batch in ended_long:
                 finish_scale(batch)
                 store(batch)
             for batch in ended:

@@ -24,6 +24,7 @@ ROW_FLOATS = BATCHES * FEATURES
 OVERHANG = 4
 EVEN_START = 248
 ODD_START = 252
+MX_ALIGN = 256
 LN_EPS = 1e-5
 LINK_EPS = 1e-8
 
@@ -78,8 +79,8 @@ def tile_embed_update_pa_t_kernel(
                 )
             x_tiles[s] = x_rows
 
-        w1_scales_raw = const.tile([P, IN_PASSES, HID], U8, align_bytes=64)
-        wf_scales = const.tile([P, CHANNELS], U8, align_bytes=64)
+        w1_scales_raw = const.tile([P, IN_PASSES, HID], U8, align_bytes=MX_ALIGN)
+        wf_scales = const.tile([P, CHANNELS], U8, align_bytes=MX_ALIGN)
         nc.vector.memset(w1_scales_raw[:].rearrange("p g n -> p (g n)").bitcast(I32), 0)
         nc.vector.memset(wf_scales[:].bitcast(I32), 0)
 
@@ -93,14 +94,14 @@ def tile_embed_update_pa_t_kernel(
         load_x(0, PAIRS)
         load_scales(w1_scales_raw, W1_scales.rearrange("g r n -> r g n"))
         load_x(1, PAIRS)
-        w1_raw = const.tile([P, IN_PASSES, HID], I32, align_bytes=64)
+        w1_raw = const.tile([P, IN_PASSES, HID], I32, align_bytes=MX_ALIGN)
         nc.sync.dma_start(
             out=w1_raw[:], in_=W1_words.rearrange("g p n t -> p g (n t)").bitcast(I32)
         )
         b1_bf = const.tile([P, PACK], BF16)
         nc.sync.dma_start(out=b1_bf[:], in_=b1.rearrange("(p t) -> p t", t=PACK))
         load_x(2, 1)
-        wf_words = const.tile([P, 4 * CHANNELS], U8, align_bytes=64)
+        wf_words = const.tile([P, 4 * CHANNELS], U8, align_bytes=MX_ALIGN)
         nc.sync.dma_start(
             out=wf_words[:].bitcast(I32), in_=Wf_words[0].rearrange("p n t -> p (n t)").bitcast(I32)
         )
@@ -120,13 +121,13 @@ def tile_embed_update_pa_t_kernel(
         for s in range(5, X_BUFS):
             load_x(s, 1)
 
-        w1_words = const.tile([P, IN_PASSES, PACK, P], I32, align_bytes=64)
-        w1_scales = const.tile([P, IN_PASSES, PACK, P], U8, align_bytes=64)
+        w1_words = const.tile([P, IN_PASSES, PACK, P], I32, align_bytes=MX_ALIGN)
+        w1_scales = const.tile([P, IN_PASSES, PACK, MX_ALIGN], U8, align_bytes=MX_ALIGN)
 
         def reorder_w1_scales():
             for g in range(IN_PASSES):
                 nc.vector.tensor_copy(
-                    out=w1_scales[:, g], in_=w1_scales_raw[:, g, :].rearrange("p (c t) -> p t c", t=PACK)
+                    out=w1_scales[:, g, :, 0:P], in_=w1_scales_raw[:, g, :].rearrange("p (c t) -> p t c", t=PACK)
                 )
 
         def reorder_w1_words():
@@ -162,15 +163,15 @@ def tile_embed_update_pa_t_kernel(
                 xt_tiles[s, pair, g] = x_t
 
         def group_x(s):
-            x_grouped = stage.tile([P, IN_PASSES, GROUP_TILES, P, PACK], BF16, align_bytes=64)
+            x_grouped = stage.tile([P, IN_PASSES, GROUP_TILES, P, PACK], BF16, align_bytes=MX_ALIGN)
             for pair, g in banks(s):
                 nc.scalar.copy(
                     out=x_grouped[:, g, 2 * pair : 2 * pair + 2].bitcast(F32),
                     in_=xt_tiles[s, pair, g][:].rearrange("p j u t -> p j t u"),
                 )
             xg_tiles[s] = x_grouped
-            x_codes = stage.tile([P, IN_PASSES, GROUP_TILES, P], U32, align_bytes=64)
-            x_scales = stage.tile([P, IN_PASSES, GROUP_TILES, P], U8, align_bytes=64)
+            x_codes = stage.tile([P, IN_PASSES, GROUP_TILES, P], U32, align_bytes=MX_ALIGN)
+            x_scales = stage.tile([P, IN_PASSES, GROUP_TILES, P], U8, align_bytes=MX_ALIGN)
             xq_tiles[s] = (x_codes, x_scales)
 
         def quantise_x(s, g, tiles=slice(0, GROUP_TILES)):
@@ -197,7 +198,7 @@ def tile_embed_update_pa_t_kernel(
                     nc.tensor.matmul_mx(
                         out=acc[:],
                         lhsT=w1_words[:, g, t, :].bitcast(FP8X4),
-                        lhsT_scale=w1_scales[:, g, t, :],
+                        lhsT_scale=w1_scales[:, g, t, 0:P],
                         rhs=x_codes[:, g, first : first + tiles].rearrange("p j t -> p (j t)").bitcast(FP8X4),
                         rhs_scale=x_scales[:, g, first : first + tiles].rearrange("p j t -> p (j t)"),
                         start=(g == 0),
@@ -209,7 +210,7 @@ def tile_embed_update_pa_t_kernel(
             hf_tiles[u] = h_flat
 
         def interleave_h(u):
-            h_grouped = stage.tile([P, UNITS[u][2] * P, PACK], BF16, align_bytes=64)
+            h_grouped = stage.tile([P, UNITS[u][2] * P, PACK], BF16, align_bytes=MX_ALIGN)
             nc.vector.tensor_copy(
                 out=h_grouped[:].rearrange("p (c i) t -> p c t i", i=4),
                 in_=hf_tiles[u][:].rearrange("p t (c i) -> p c t i", i=4),
@@ -217,8 +218,8 @@ def tile_embed_update_pa_t_kernel(
             hg_tiles[u] = h_grouped
 
         def quantise_h(u):
-            h_codes = stage.tile([P, UNITS[u][2], P], U32, align_bytes=64)
-            h_scales = stage.tile([P, UNITS[u][2], P], U8, align_bytes=64)
+            h_codes = stage.tile([P, UNITS[u][2], P], U32, align_bytes=MX_ALIGN)
+            h_scales = stage.tile([P, UNITS[u][2], P], U8, align_bytes=MX_ALIGN)
             nc.vector.quantize_mx(
                 out=h_codes[:].rearrange("p j t -> p (j t)").bitcast(FP8X4),
                 scales=h_scales[:].rearrange("p j t -> p (j t)"),
@@ -267,7 +268,7 @@ def tile_embed_update_pa_t_kernel(
             column = columns(u).start + j
             batch, link = divmod(column, LINKS)
             weight = last_lm[:, link : link + 1] if u == D else terms[:, L_M, column : column + 1]
-            sums_of_batch = 1 if u >= WHOLE - 1 else 2
+            sums_of_batch = 1 if batch == BATCHES - 1 else 2
             if link < sums_of_batch:
                 link_sum = finish_pool.tile([P, CHANNELS], F32, tag="link_sum%d" % link)
                 nc.vector.tensor_scalar(
@@ -544,6 +545,7 @@ def tile_embed_update_pa_t_kernel(
                 finish_lg(ended)
             if i >= 2:
                 add_link(i - 2, 0)
+            if 2 <= i < WHOLE:
                 add_link(i - 2, 1)
             if ended_before:
                 finish_aggregate(ended_before)
@@ -551,6 +553,8 @@ def tile_embed_update_pa_t_kernel(
                 finish_sums(ended)
             if i >= 1:
                 quantise_x(i + 1, 1)
+            if i == WHOLE:
+                add_link(i - 2, 1)
             for batch in ended_before:
                 finish_centre(batch)
             if ended:
@@ -579,9 +583,9 @@ def tile_embed_update_pa_t_kernel(
         gate(U)
         interleave_h(A)
         add_link(U - 1, 2)
-        add_link(U - 1, 3)
         quantise_h(A)
         first_matmul(C)
+        add_link(U - 1, 3)
         interleave_h(B)
         link_gate(columns(U))
         quantise_h(B)
@@ -593,7 +597,6 @@ def tile_embed_update_pa_t_kernel(
         gate(B)
         interleave_h(C)
         finish_bias(last - 1)
-        last_merge(last)
         quantise_h(C)
         second_matmul(C, from_ring=True)
         for j in range(GROUP_TILES):

from contextlib import ExitStack

import concourse.mybir as mybir
from concourse.masks import make_identity

F32 = mybir.dt.float32
BF16 = mybir.dt.bfloat16
I32 = mybir.dt.int32
U8 = mybir.dt.uint8
U32 = mybir.dt.uint32
FP8X4 = mybir.dt.float8_e4m3fn_x4
ALU = mybir.AluOpType
ACT = mybir.ActivationFunctionType
AXIS = mybir.AxisListType

P = 128
BATCHES, LINKS, IN, HID, CHANNELS = 4, 16, 1024, 512, 128
FEATURES = CHANNELS - 1
PACK = 4
K_PASS = PACK * P
PASS_WORDS = K_PASS // 2
IN_PASSES = IN // K_PASS
ROW_FLOATS = BATCHES * FEATURES
OVERHANG = 4
EVEN_START = 248
ODD_START = 252
MX_ALIGN = 256
LN_EPS = 1e-5
LINK_EPS = 1e-8

GROUP_TILES = 4
GROUP_ROWS = GROUP_TILES * P
GROUPS = BATCHES * LINKS // GROUP_TILES
GROUPS_PER_BATCH = LINKS // GROUP_TILES
PAIRS = GROUP_TILES // 2
X_BUFS = 8
SPLIT_GROUPS = 2
UNITS = [(s, 0, GROUP_TILES) for s in range(GROUPS - SPLIT_GROUPS)] + [
    (s, j, GROUP_TILES // 2) for s in range(GROUPS - SPLIT_GROUPS, GROUPS) for j in (0, GROUP_TILES // 2)
]

FLOPS = 2 * BATCHES * P * LINKS * (IN * HID + HID * CHANNELS)


def tile_embed_update_pa_t_kernel(
    tc, net_in, embeds, m, W1_words, W1_scales, b1, Wf_words, Wf_scales, b_f, gamma, beta, out
):
    nc = tc.nc
    net_in_rows = net_in.rearrange("b s k i -> (b s) k i").rearrange("(p b) k i -> b p k i", b=BATCHES)
    out_rows = out.rearrange("b s c -> (b s c)").rearrange("(p f) -> p f", p=P)
    out_pairs = out.rearrange("b s c -> (b s c)").rearrange("(q f) -> q f", q=P // 2)
    with ExitStack() as ctx:
        ctx.enter_context(tc.manual_schedule())
        const = ctx.enter_context(tc.tile_pool(name="const", bufs=1))
        x_pool = ctx.enter_context(tc.tile_pool(name="x", bufs=X_BUFS))
        stage = ctx.enter_context(tc.tile_pool(name="stage", bufs=2))
        finish_pool = ctx.enter_context(tc.tile_pool(name="finish", bufs=2))
        psum = ctx.enter_context(tc.psum_pool(name="psum", bufs=6))
        o_pool = ctx.enter_context(tc.psum_pool(name="o", bufs=2))

        identity = const.tile([P, P], F32)
        make_identity(nc, identity[:])
        minus_half = const.tile([P, 2], F32)
        nc.gpsimd.memset(minus_half[:], -0.5)
        table_warmer = const.tile([P, 1], F32)
        nc.scalar.activation(out=table_warmer[:], in_=minus_half[:, 0:1], func=ACT.Sigmoid)

        x_tiles = {}

        def load_x(s, pieces):
            batch, quarter = divmod(s, GROUPS_PER_BATCH)
            first_link = quarter * GROUP_TILES
            x_rows = x_pool.tile([P, GROUP_TILES, IN], BF16)
            step = GROUP_TILES // pieces
            for h in range(pieces):
                nc.sync.dma_start(
                    out=x_rows[:, h * step : (h + 1) * step, :],
                    in_=net_in_rows[batch, :, first_link + h * step : first_link + (h + 1) * step, :],
                )
            x_tiles[s] = x_rows

        w1_scales_raw = const.tile([P, IN_PASSES, HID], U8, align_bytes=MX_ALIGN)
        wf_scales = const.tile([P, CHANNELS], U8, align_bytes=MX_ALIGN)
        nc.vector.memset(w1_scales_raw[:].rearrange("p g n -> p (g n)").bitcast(I32), 0)
        nc.vector.memset(wf_scales[:].bitcast(I32), 0)

        def load_scales(scale_tile, scale_rows):
            for quadrant in range(4):
                nc.sync.dma_start(
                    out=scale_tile[32 * quadrant : 32 * quadrant + 4].bitcast(I32),
                    in_=scale_rows[4 * quadrant : 4 * quadrant + 4].bitcast(I32),
                )

        load_x(0, PAIRS)
        load_scales(w1_scales_raw, W1_scales.rearrange("g r n -> r g n"))
        load_x(1, PAIRS)
        w1_raw = const.tile([P, IN_PASSES, HID], I32, align_bytes=MX_ALIGN)
        nc.sync.dma_start(
            out=w1_raw[:], in_=W1_words.rearrange("g p n t -> p g (n t)").bitcast(I32)
        )
        b1_bf = const.tile([P, PACK], BF16)
        nc.sync.dma_start(out=b1_bf[:], in_=b1.rearrange("(p t) -> p t", t=PACK))
        load_x(2, 1)
        wf_words = const.tile([P, 4 * CHANNELS], U8, align_bytes=MX_ALIGN)
        nc.sync.dma_start(
            out=wf_words[:].bitcast(I32), in_=Wf_words[0].rearrange("p n t -> p (n t)").bitcast(I32)
        )
        load_scales(wf_scales, Wf_scales[0])
        bf_bf = const.tile([P, CHANNELS], BF16)
        nc.sync.dma_start(out=bf_bf[:], in_=b_f.partition_broadcast(P))
        m_bf = const.tile([P, BATCHES, LINKS], BF16)
        nc.sync.dma_start(out=m_bf[:], in_=m.rearrange("b s k o -> (b s) (k o)").rearrange("(p b) k -> p b k", b=BATCHES))
        load_x(3, 1)
        load_x(4, 1)
        gamma_bf = const.tile([P, FEATURES], BF16)
        nc.sync.dma_start(out=gamma_bf[:], in_=gamma.partition_broadcast(P))
        beta_bf = const.tile([P, FEATURES], BF16)
        nc.sync.dma_start(out=beta_bf[:], in_=beta.partition_broadcast(P))
        embeds_bf = const.tile([P, BATCHES, FEATURES], BF16)
        nc.sync.dma_start(out=embeds_bf[:], in_=embeds.rearrange("b s c -> (b s) c").rearrange("(p b) c -> p b c", b=BATCHES))
        for s in range(5, X_BUFS):
            load_x(s, 1)

        w1_words = const.tile([P, IN_PASSES, PACK, P], I32, align_bytes=MX_ALIGN)
        w1_scales = const.tile([P, IN_PASSES, PACK, MX_ALIGN], U8, align_bytes=MX_ALIGN)

        def reorder_w1_scales():
            for g in range(IN_PASSES):
                nc.vector.tensor_copy(
                    out=w1_scales[:, g, :, 0:P], in_=w1_scales_raw[:, g, :].rearrange("p (c t) -> p t c", t=PACK)
                )

        def reorder_w1_words():
            for t in range(PACK):
                nc.vector.tensor_copy(
                    out=w1_words[:, :, t, :], in_=w1_raw[:].rearrange("p g (c t) -> p g c t", t=PACK)[:, :, :, t]
                )

        m_link = m_bf[:].rearrange("s b k -> s (b k)")
        sigmoid = const.tile([P, BATCHES * LINKS], F32)
        g_link = const.tile([P, BATCHES * LINKS], F32)
        L, L_M, L_G = 0, 1, 2
        terms = const.tile([P, 3, BATCHES * LINKS], F32)

        xt_tiles, xg_tiles, xq_tiles = {}, {}, {}

        def banks(s):
            if s < 2:
                return [(pair, g) for pair in range(PAIRS) for g in range(IN_PASSES)]
            return [(pair, g) for g in range(IN_PASSES) for pair in range(PAIRS)]

        def transpose_x(s):
            for pair, g in banks(s):
                x_t = psum.tile([P, 2, 2, P], F32, tag="bank")
                for j in range(2):
                    words = x_tiles[s][:, 2 * pair + j, :].bitcast(F32)
                    for u in range(2):
                        nc.tensor.transpose(
                            x_t[:, j, u, :],
                            words[:, g * PASS_WORDS + u : (g + 1) * PASS_WORDS : 2],
                            identity[:],
                        )
                xt_tiles[s, pair, g] = x_t

        def group_x(s):
            x_grouped = stage.tile([P, IN_PASSES, GROUP_TILES, P, PACK], BF16, align_bytes=MX_ALIGN)
            for pair, g in banks(s):
                nc.scalar.copy(
                    out=x_grouped[:, g, 2 * pair : 2 * pair + 2].bitcast(F32),
                    in_=xt_tiles[s, pair, g][:].rearrange("p j u t -> p j t u"),
                )
            xg_tiles[s] = x_grouped
            x_codes = stage.tile([P, IN_PASSES, GROUP_TILES, P], U32, align_bytes=MX_ALIGN)
            x_scales = stage.tile([P, IN_PASSES, GROUP_TILES, P], U8, align_bytes=MX_ALIGN)
            xq_tiles[s] = (x_codes, x_scales)

        def quantise_x(s, g, tiles=slice(0, GROUP_TILES)):
            x_codes, x_scales = xq_tiles[s]
            nc.vector.quantize_mx(
                out=x_codes[:, g, tiles].rearrange("p j t -> p (j t)").bitcast(FP8X4),
                scales=x_scales[:, g, tiles].rearrange("p j t -> p (j t)"),
                in_=xg_tiles[s][:, g, tiles].rearrange("p j t e -> p (j t e)"),
            )

        hf_tiles, hg_tiles, hq_tiles, o_tiles, sum_tiles = {}, {}, {}, {}, {}

        def columns(u):
            s, first, tiles = UNITS[u]
            return slice(s * GROUP_TILES + first, s * GROUP_TILES + first + tiles)

        def first_matmul(u):
            s, first, tiles = UNITS[u]
            x_codes, x_scales = xq_tiles[s]
            h_flat = stage.tile([P, PACK, tiles * P], BF16)
            for t in range(PACK):
                acc = psum.tile([P, tiles * P], F32, tag="bank")
                for g in range(IN_PASSES):
                    nc.tensor.matmul_mx(
                        out=acc[:],
                        lhsT=w1_words[:, g, t, :].bitcast(FP8X4),
                        lhsT_scale=w1_scales[:, g, t, 0:P],
                        rhs=x_codes[:, g, first : first + tiles].rearrange("p j t -> p (j t)").bitcast(FP8X4),
                        rhs_scale=x_scales[:, g, first : first + tiles].rearrange("p j t -> p (j t)"),
                        start=(g == 0),
                        stop=(g == IN_PASSES - 1),
                    )
                nc.scalar.activation(
                    out=h_flat[:, t, :], in_=acc[:], func=ACT.Relu, bias=b1_bf[:, t : t + 1]
                )
            hf_tiles[u] = h_flat

        def interleave_h(u):
            h_grouped = stage.tile([P, UNITS[u][2] * P, PACK], BF16, align_bytes=MX_ALIGN)
            nc.vector.tensor_copy(
                out=h_grouped[:].rearrange("p (c i) t -> p c t i", i=4),
                in_=hf_tiles[u][:].rearrange("p t (c i) -> p c t i", i=4),
            )
            hg_tiles[u] = h_grouped

        def quantise_h(u):
            h_codes = stage.tile([P, UNITS[u][2], P], U32, align_bytes=MX_ALIGN)
            h_scales = stage.tile([P, UNITS[u][2], P], U8, align_bytes=MX_ALIGN)
            nc.vector.quantize_mx(
                out=h_codes[:].rearrange("p j t -> p (j t)").bitcast(FP8X4),
                scales=h_scales[:].rearrange("p j t -> p (j t)"),
                in_=hg_tiles[u][:].rearrange("p n t -> p (n t)"),
            )
            hq_tiles[u] = (h_codes, h_scales)

        def second_matmul(u, from_ring=False):
            h_codes, h_scales = hq_tiles[u]
            if from_ring:
                o = psum.tile([P, UNITS[u][2], CHANNELS], F32, tag="bank")
            else:
                o = o_pool.tile([P, UNITS[u][2], CHANNELS], F32)
            for j in range(UNITS[u][2]):
                nc.tensor.matmul_mx(
                    out=o[:, j, :],
                    lhsT=h_codes[:, j, :].bitcast(FP8X4),
                    lhsT_scale=h_scales[:, j, :],
                    rhs=wf_words[:].bitcast(FP8X4),
                    rhs_scale=wf_scales[:],
                    start=True,
                    stop=True,
                )
            o_tiles[u] = o

        def gate(u):
            nc.scalar.activation(
                out=sigmoid[:, columns(u)],
                in_=o_tiles[u][:, :, FEATURES],
                func=ACT.Sigmoid,
                bias=bf_bf[:, FEATURES:CHANNELS],
            )

        def link_gate(cols):
            nc.vector.tensor_tensor(
                out=g_link[:, cols], in0=sigmoid[:, cols], in1=m_link[:, cols], op=ALU.mult
            )

        def link_weight(cols):
            nc.vector.scalar_tensor_tensor(
                out=terms[:, L_M, cols], in0=g_link[:, cols], scalar=LINK_EPS, in1=m_link[:, cols],
                op0=ALU.add, op1=ALU.mult,
            )

        def add_link(u, j):
            column = columns(u).start + j
            batch, link = divmod(column, LINKS)
            weight = last_lm[:, link : link + 1] if u == D else terms[:, L_M, column : column + 1]
            sums_of_batch = 1 if batch == BATCHES - 1 else 2
            if link < sums_of_batch:
                link_sum = finish_pool.tile([P, CHANNELS], F32, tag="link_sum%d" % link)
                nc.vector.tensor_scalar(
                    out=link_sum[:], in0=o_tiles[u][:, j, :], scalar1=weight, scalar2=None, op0=ALU.mult
                )
                sum_tiles[batch, link] = link_sum
            else:
                link_sum = sum_tiles[batch, link % sums_of_batch]
                nc.vector.scalar_tensor_tensor(
                    out=link_sum[:], in0=o_tiles[u][:, j, :], scalar=weight, in1=link_sum[:],
                    op0=ALU.mult, op1=ALU.add,
                )

        scaled_tiles = []

        def scale_link(u, j):
            scaled = finish_pool.tile([P, CHANNELS], F32, bufs=6)
            column = columns(u).start + j
            nc.scalar.activation(
                out=scaled[:], in_=o_tiles[u][:, j, :], func=ACT.Copy, scale=terms[:, L_M, column : column + 1]
            )
            scaled_tiles.append(scaled)

        def sum_scaled(first, last):
            for n, scaled in enumerate(scaled_tiles):
                nc.tensor.matmul(
                    out=tensor_sum[:], lhsT=identity[:], rhs=scaled[:],
                    start=first and n == 0, stop=last and n == len(scaled_tiles) - 1,
                )
            scaled_tiles.clear()

        sums_tiles, factor_tiles, e_tiles, norm_tiles = {}, {}, {}, {}
        result = const.tile([P, ROW_FLOATS + OVERHANG], F32)

        def batch_columns(batches):
            return slice(batches[0] * LINKS, (batches[-1] + 1) * LINKS)

        def finish_l(batches):
            cols = batch_columns(batches)
            nc.vector.tensor_scalar(
                out=terms[:, L, cols], in0=g_link[:, cols], scalar1=LINK_EPS, scalar2=None, op0=ALU.add
            )

        def finish_lg(batches):
            cols = batch_columns(batches)
            nc.vector.tensor_tensor(
                out=terms[:, L_G, cols], in0=terms[:, L, cols], in1=g_link[:, cols], op=ALU.mult
            )

        def finish_sums(batches):
            sums = finish_pool.tile([P, 3, len(batches)], F32)
            nc.vector.tensor_reduce(
                out=sums[:], in_=terms[:, :, batch_columns(batches)].rearrange("p k (b l) -> p k b l", l=LINKS),
                axis=AXIS.X, op=ALU.add,
            )
            for k, batch in enumerate(batches):
                sums_tiles[batch] = (sums, k)

        def finish_invert(batches):
            inv_l = finish_pool.tile([P, len(batches)], F32)
            nc.vector.reciprocal(out=inv_l[:], in_=sums_tiles[batches[0]][0][:, L, :])
            for k, batch in enumerate(batches):
                factor_tiles[batch] = inv_l[:, k : k + 1]

        def last_gates(batch):
            cols = batch_columns([batch])
            nc.vector.scalar_tensor_tensor(
                out=last_g[:], in0=sigmoid[:, cols], scalar=1.0, in1=m_link[:, cols],
                op0=ALU.mult, op1=ALU.mult, accum_out=last_sums[:, 0:1],
            )

        def last_weights(batch):
            cols = batch_columns([batch])
            nc.vector.scalar_tensor_tensor(
                out=last_lm[:], in0=last_g[:], scalar=LINK_EPS, in1=m_link[:, cols],
                op0=ALU.add, op1=ALU.mult, accum_out=last_sums[:, 1:2],
            )

        def last_l(batch):
            nc.vector.tensor_scalar(
                out=last_sums[:, 3:4], in0=last_sums[:, 0:1], scalar1=LINKS * LINK_EPS, scalar2=None, op0=ALU.add
            )

        def last_squares(batch):
            cols = batch_columns([batch])
            nc.vector.scalar_tensor_tensor(
                out=last_lg[:], in0=last_g[:], scalar=LINK_EPS, in1=last_g[:],
                op0=ALU.add, op1=ALU.mult, accum_out=last_sums[:, 2:3],
            )

        def last_invert(batch):
            nc.vector.reciprocal(out=last_sums[:, 4:5], in_=last_sums[:, 3:4])

        def last_factor(batch):
            nc.vector.tensor_scalar(
                out=last_sums[:, 5:6], in0=last_sums[:, 2:3], scalar1=last_sums[:, 4:5], scalar2=last_sums[:, 4:5],
                op0=ALU.mult, op1=ALU.mult,
            )
            factor_tiles[batch] = last_sums[:, 5:6]

        def last_bias(batch):
            biased = finish_pool.tile([P, FEATURES], F32)
            nc.vector.scalar_tensor_tensor(
                out=biased[:], in0=bf_bf[:, 0:FEATURES], scalar=last_sums[:, 1:2],
                in1=sum_tiles[batch, 0][:, 0:FEATURES], op0=ALU.mult, op1=ALU.add,
            )
            e_tiles[batch] = biased

        def last_tensor_part(batch):
            part = finish_pool.tile([P, FEATURES], F32)
            nc.vector.scalar_tensor_tensor(
                out=part[:], in0=tensor_sum[:, 0:FEATURES], scalar=factor_tiles[batch], in1=embeds_bf[:, batch, :],
                op0=ALU.mult, op1=ALU.add,
            )
            sum_tiles[batch, 2] = part

        def last_e(batch):
            e = finish_pool.tile([P, FEATURES], F32)
            nc.vector.scalar_tensor_tensor(
                out=e[:], in0=e_tiles[batch][:], scalar=factor_tiles[batch], in1=sum_tiles[batch, 2][:],
                op0=ALU.mult, op1=ALU.add,
            )
            e_tiles[batch] = e

        def last_merge(batch):
            nc.vector.tensor_tensor(
                out=sum_tiles[batch, 0][:], in0=sum_tiles[batch, 0][:], in1=sum_tiles[batch, 1][:], op=ALU.add
            )

        last_sums = const.tile([P, 6], F32)
        last_g = const.tile([P, LINKS], F32)
        last_lm = const.tile([P, LINKS], F32)
        last_lg = const.tile([P, LINKS], F32)

        def finish_factor(batch):
            sums, k = sums_tiles[batch]
            inv_l = factor_tiles[batch]
            factor = finish_pool.tile([P, 1], F32)
            nc.vector.tensor_scalar(
                out=factor[:], in0=sums[:, L_G, k : k + 1], scalar1=inv_l, scalar2=inv_l, op0=ALU.mult, op1=ALU.mult
            )
            factor_tiles[batch] = factor[:]

        def finish_bias(batch):
            biased = finish_pool.tile([P, FEATURES], F32)
            link_sum = e_tiles[batch]
            nc.vector.scalar_tensor_tensor(
                out=biased[:], in0=bf_bf[:, 0:FEATURES],
                scalar=sums_tiles[batch][0][:, L_M, sums_tiles[batch][1] : sums_tiles[batch][1] + 1],
                in1=link_sum[:, 0:FEATURES], op0=ALU.mult, op1=ALU.add,
            )
            e_tiles[batch] = biased

        def finish_update(batch):
            update = finish_pool.tile([P, FEATURES], F32)
            nc.vector.tensor_tensor(
                out=update[:], in0=sum_tiles[batch, 0][:, 0:FEATURES], in1=sum_tiles[batch, 1][:, 0:FEATURES], op=ALU.add
            )
            e_tiles[batch] = update

        def finish_e(batch):
            e = finish_pool.tile([P, FEATURES], F32)
            nc.vector.scalar_tensor_tensor(
                out=e[:], in0=e_tiles[batch][:], scalar=factor_tiles[batch], in1=embeds_bf[:, batch, :],
                op0=ALU.mult, op1=ALU.add,
            )
            e_tiles[batch] = e

        def finish_stats(batch):
            stats = finish_pool.tile([P, 6], F32)
            nc.vector.bn_stats(out=stats[:], in_=e_tiles[batch][:])
            norm_tiles[batch] = stats

        def finish_aggregate(batches, on_scalar=False):
            n = len(batches)
            mean_var = finish_pool.tile([P, n, 2], F32)
            for k, batch in enumerate(batches):
                nc.vector.bn_aggr(out=mean_var[:, k, :], in_=norm_tiles[batch][:])
            if on_scalar:
                inv_std = finish_pool.tile([P, n], F32)
                nc.scalar.activation(
                    out=inv_std[:], in_=mean_var[:, :, 1], func=ACT.Abs_reciprocal_sqrt, bias=LN_EPS
                )
                for k, batch in enumerate(batches):
                    norm_tiles[batch] = (mean_var[:, k, 0:1], inv_std[:, k : k + 1])
                return
            var_eps = finish_pool.tile([P, n], F32)
            nc.gpsimd.tensor_scalar(
                out=var_eps[:], in0=mean_var[:, :, 1], scalar1=LN_EPS, scalar2=1.0, op0=ALU.add, op1=ALU.mult
            )
            inv_std = finish_pool.tile([P, n], F32)
            nc.gpsimd.tensor_tensor(out=inv_std[:], in0=var_eps[:], in1=minus_half[:, 0:n], op=ALU.pow)
            for k, batch in enumerate(batches):
                norm_tiles[batch] = (mean_var[:, k, 0:1], inv_std[:, k : k + 1])

        def finish_centre(batch):
            centred = finish_pool.tile([P, FEATURES], F32)
            nc.vector.scalar_tensor_tensor(
                out=centred[:], in0=e_tiles[batch][:], scalar=norm_tiles[batch][0], in1=gamma_bf[:],
                op0=ALU.subtract, op1=ALU.mult,
            )
            e_tiles[batch] = centred

        def finish_scale(batch):
            nc.vector.scalar_tensor_tensor(
                out=result[:, batch * FEATURES : (batch + 1) * FEATURES], in0=e_tiles[batch][:], scalar=norm_tiles[batch][1], in1=beta_bf[:],
                op0=ALU.mult, op1=ALU.add,
            )

        def store(batch):
            cols = slice(batch * FEATURES, (batch + 1) * FEATURES)
            nc.sync.dma_start(out=out_rows[:, cols], in_=result[:, cols])

        def fetch_overhang():
            nc.sync.dma_start(
                out=result[0::2, ROW_FLOATS:], in_=out_pairs[:, ROW_FLOATS : ROW_FLOATS + OVERHANG]
            )

        def store_last_two():
            nc.sync.dma_start(out=out_pairs[:, EVEN_START : ROW_FLOATS + OVERHANG], in_=result[0::2, EVEN_START:])
            nc.scalar.dma_start(
                out=out_pairs[:, ROW_FLOATS + ODD_START :], in_=result[1::2, ODD_START:ROW_FLOATS]
            )

        WHOLE = GROUPS - SPLIT_GROUPS
        A, B, C, D = WHOLE, WHOLE + 1, WHOLE + 2, WHOLE + 3

        def batch_of(u):
            return columns(u).start // LINKS

        def ends_batch(u):
            return u >= 0 and columns(u).stop % LINKS == 0 and batch_of(u) < BATCHES - 1

        transpose_x(0)
        group_x(0)
        for pair, g in banks(0):
            quantise_x(0, g, slice(2 * pair, 2 * pair + 2))
        reorder_w1_scales()

        reorder_w1_words()

        for i in range(WHOLE + 1):
            if i >= 2:
                gate(i - 2)
            transpose_x(i + 1)
            group_x(i + 1)
            if i + X_BUFS < GROUPS:
                load_x(i + X_BUFS, 1)
            ended = [batch_of(i - 2)] if ends_batch(i - 2) else []
            ended_before = [batch_of(i - 3)] if ends_batch(i - 3) and i < WHOLE else []
            ended_long = [batch_of(i - 4)] if ends_batch(i - 4) else []
            if i >= 1:
                interleave_h(i - 1)
            if i >= 2:
                link_gate(columns(i - 2))
            for batch in ended_before:
                finish_bias(batch)
            if i == 0:
                for pair, g in banks(1):
                    quantise_x(1, g, slice(2 * pair, 2 * pair + 2))
            else:
                quantise_x(i + 1, 0)
            if i >= 2:
                link_weight(columns(i - 2))
            for batch in ended_before:
                finish_e(batch)
            if ended:
                finish_l(ended)
            if i >= 1:
                quantise_h(i - 1)
            for batch in ended_before:
                finish_stats(batch)
            if ended:
                finish_lg(ended)
            if i >= 2:
                add_link(i - 2, 0)
            if 2 <= i < WHOLE:
                add_link(i - 2, 1)
            if ended_before:
                finish_aggregate(ended_before)
            if ended:
                finish_sums(ended)
            if i >= 1:
                quantise_x(i + 1, 1)
            if i == WHOLE:
                add_link(i - 2, 1)
            for batch in ended_before:
                finish_centre(batch)
            if ended:
                finish_invert(ended)
            if 2 <= i < WHOLE:
                add_link(i - 2, 2)
                add_link(i - 2, 3)
            for batch in ended_long:
                finish_scale(batch)
                store(batch)
            for batch in ended:
                finish_factor(batch)
                finish_update(batch)
            if i == GROUPS // 2:
                fetch_overhang()
            if i < WHOLE:
                first_matmul(i)
            else:
                first_matmul(A)
                first_matmul(B)
            if i >= 1:
                second_matmul(i - 1)

        last = BATCHES - 1
        U = WHOLE - 1
        gate(U)
        interleave_h(A)
        add_link(U - 1, 2)
        quantise_h(A)
        first_matmul(C)
        add_link(U - 1, 3)
        interleave_h(B)
        link_gate(columns(U))
        quantise_h(B)
        link_weight(columns(U))
        first_matmul(D)
        second_matmul(A, from_ring=True)
        gate(A)
        second_matmul(B, from_ring=True)
        gate(B)
        interleave_h(C)
        finish_bias(last - 1)
        quantise_h(C)
        second_matmul(C, from_ring=True)
        for j in range(GROUP_TILES):
            scale_link(U, j)
        gate(C)
        tensor_sum = psum.tile([P, CHANNELS], F32, tag="bank")
        sum_scaled(True, False)
        interleave_h(D)
        link_gate(slice(columns(A).start, columns(B).stop))
        quantise_h(D)
        second_matmul(D, from_ring=True)
        link_weight(slice(columns(A).start, columns(B).stop))
        link_gate(columns(C))
        scale_link(A, 0)
        scale_link(A, 1)
        gate(D)
        finish_e(last - 1)
        link_weight(columns(C))
        for u, j in ((B, 0), (B, 1), (C, 0), (C, 1)):
            scale_link(u, j)
        nc.scalar.activation(out=table_warmer[:], in_=minus_half[:, 0:1], func=ACT.Abs_reciprocal_sqrt)
        sum_scaled(False, True)
        last_gates(last)
        finish_stats(last - 1)
        last_weights(last)
        last_l(last)
        last_squares(last)
        add_link(D, 0)
        last_invert(last)
        add_link(D, 1)
        last_factor(last)
        finish_aggregate([last - 1], on_scalar=True)
        last_tensor_part(last)
        last_bias(last)
        finish_centre(last - 1)
        last_e(last)
        finish_scale(last - 1)
        finish_stats(last)
        finish_aggregate([last], on_scalar=True)
        finish_centre(last)
        finish_scale(last)
        store_last_two()
